import numpy as np
import ml_dtypes


def mxq(x, axis, fmt="e4m3"):
    dtype, down = {"e4m3": (ml_dtypes.float8_e4m3fn, 7), "e5m2": (ml_dtypes.float8_e5m2, 14)}[fmt]
    v = np.moveaxis(np.asarray(x, np.float32).astype(ml_dtypes.bfloat16).astype(np.float64), axis, -1)
    blocks = v.reshape(v.shape[:-1] + (-1, 32))
    amax = np.abs(blocks).max(-1, keepdims=True)
    byte = np.maximum(np.where(amax > 0, np.frexp(amax)[1] - 1 + 127, 0) - down, 1)
    scale = np.exp2(byte - 127.0)
    codes = (blocks / scale).astype(np.float32).astype(dtype).astype(np.float64)
    return np.moveaxis((codes * scale).reshape(v.shape), -1, axis)


WIDE = False


def mx_kscale(k):
    if not WIDE:
        return np.ones(k)
    levels = np.array([20, -20, 10, -10, 0])
    a = np.random.permutation(np.resize(levels, k // 512 * 4)).reshape(k // 512, 4)
    idx = np.arange(k)
    return np.exp2(a[idx // 512, idx % 128 // 32])


BF16 = ml_dtypes.bfloat16


def bf(x):
    return np.asarray(x, np.float32).astype(BF16)


def f64(x):
    return np.asarray(x).astype(np.float64)


L, F, O, N, B, D = 2, 512, 512, 1024, 1, 3
G = O + O + O


def sigmoid(v):
    return 1.0 / (1.0 + np.exp(-v))


def forward_parts(agg, x, wih, whh, bih, bhh, wh, bh):
    x = f64(x)
    h = x.transpose(1, 0, 2)[None]
    gi = f64(agg) @ f64(wih).T + f64(bih)
    gh = h @ f64(whh).T + f64(bhh)
    r = sigmoid(gi[..., :O] + gh[..., :O])
    z = sigmoid(gi[..., O:O + O] + gh[..., O:O + O])
    c = np.tanh(gi[..., O + O:] + r * gh[..., O + O:])
    hnew = (1.0 - z) * c + z * h
    u = np.maximum(hnew.sum(0).transpose(1, 0, 2), 0.0)
    t = np.maximum(x @ f64(wh) + f64(bh), 0.0)
    return {"y": u * t + x * (1.0 - t),
            "gates": np.concatenate([r, z, c], axis=-1),
            "hn": gh[0][..., O + O:],
            "t": t}


def setup_inputs():
    s = mx_kscale(O)
    agg = bf(np.random.standard_normal((D, B, N, O)))
    x = bf(np.random.standard_normal((N, B, F)))
    wih0 = bf(np.random.standard_normal((G, O)) * 0.7 / np.sqrt(O))
    whh = bf(np.random.standard_normal((G, O)) * 0.7 / np.sqrt(O))
    bih = bf(np.random.standard_normal(G) * 0.3)
    bhh = bf(np.random.standard_normal(G) * 0.3)
    wh = bf(np.random.standard_normal((F, O)) * 0.5 / np.sqrt(F))
    bh = bf(0.3 + np.random.standard_normal(O) * 0.2)
    g = bf(np.random.standard_normal((N, B, O)) * np.exp2(np.random.randint(-12, 1, (N, 1, 1))) * 64.0 * s)
    p = forward_parts(agg, x, wih0, whh, bih, bhh, wh, bh)
    return {"agg": agg, "x": x,
            "wih": bf(f64(wih0) / np.tile(s, 3)[:, None]),
            "whh": whh, "bih": bih, "bhh": bhh, "wh": wh, "bh": bh,
            "gates": np.asarray(p["gates"], np.float32),
            "hn": np.asarray(p["hn"], np.float32),
            "t": np.asarray(p["t"], np.float32),
            "grad_out": g}


def reference(agg, x, wih, whh, bih, bhh, wh, bh, gates, hn, t, grad_out):
    h = f64(x).transpose(1, 0, 2)[None]
    gt = f64(gates)
    r, z, c = gt[..., :O], gt[..., O:O + O], gt[..., O + O:]
    hsum = ((1.0 - z) * c + z * h).sum(0)
    ds = np.where(hsum > 0.0, (f64(grad_out) * f64(t)).transpose(1, 0, 2), 0.0)[None]
    dc = ds * (1.0 - z) * (1.0 - c * c)
    dr = dc * f64(hn)[None] * r * (1.0 - r)
    dz = ds * (h - c) * z * (1.0 - z)
    dgi = np.concatenate([dr, dz, dc], axis=-1)
    return mxq(dgi, 3, "e5m2") @ mxq(f64(wih), 0, "e4m3")

@@ -1,0 +1,292 @@
+from contextlib import ExitStack
+
+import concourse.mybir as mybir
+from concourse.masks import make_identity
+
+F32 = mybir.dt.float32
+BF16 = mybir.dt.bfloat16
+U32 = mybir.dt.uint32
+U8 = mybir.dt.uint8
+E5M2_X4 = mybir.dt.float8_e5m2_x4
+E4M3_X4 = mybir.dt.float8_e4m3fn_x4
+ALU = mybir.AluOpType
+FUNC = mybir.ActivationFunctionType
+
+P = 128
+DIRECTIONS = 3
+NODES = 1024
+FEATURES = 512
+GATES = 3
+CHUNKS = FEATURES // P
+NODE_TILES = NODES // P
+
+R_COLS = slice(0, FEATURES)
+Z_COLS = slice(FEATURES, 2 * FEATURES)
+C_COLS = slice(2 * FEATURES, 3 * FEATURES)
+
+FLOPS = 2 * DIRECTIONS * NODES * GATES * FEATURES * FEATURES
+BYTES = (
+    4 * DIRECTIONS * NODES * GATES * FEATURES
+    + 2 * 4 * NODES * FEATURES
+    + 2 * 2 * NODES * FEATURES
+    + 2 * GATES * FEATURES * FEATURES
+    + 4 * DIRECTIONS * NODES * FEATURES
+)
+
+
+def by_node(bank):
+    return bank[:].rearrange("p t n -> p n t")
+
+
+def tile_graphconvolution_pb_v_kernel(
+    tc, agg, x, wih, whh, bih, bhh, wh, bh, gates, hn, t, grad_out, out
+):
+    nc = tc.nc
+    with ExitStack() as ctx:
+        once = ctx.enter_context(tc.tile_pool(name="once", bufs=1))
+        two = ctx.enter_context(tc.tile_pool(name="two", bufs=2))
+        three = ctx.enter_context(tc.tile_pool(name="three", bufs=DIRECTIONS))
+        six = ctx.enter_context(tc.tile_pool(name="six", bufs=2 * DIRECTIONS))
+        psum = ctx.enter_context(tc.psum_pool(name="psum", bufs=1))
+
+        identity = once.tile([P, P], F32, name="identity")
+        make_identity(nc, identity[:])
+
+        loaded = {}
+        prepared = {}
+        banks = {}
+        state = {}
+
+        def load(i):
+            rows = slice(i * P, (i + 1) * P)
+            x_rows = two.tile([P, FEATURES], BF16, name="x_rows")
+            nc.sync.dma_start(out=x_rows[:], in_=x[rows, 0, :])
+            gate_rows = []
+            for d in range(DIRECTIONS):
+                rzc = six.tile([P, GATES * FEATURES], F32, name="gate_rows")
+                nc.sync.dma_start(out=rzc[:], in_=gates[d, 0, rows, :])
+                gate_rows.append(rzc)
+            grad_rows = two.tile([P, FEATURES], BF16, name="grad_rows")
+            nc.sync.dma_start(out=grad_rows[:], in_=grad_out[rows, 0, :])
+            t_rows = two.tile([P, FEATURES], F32, name="t_rows")
+            nc.sync.dma_start(out=t_rows[:], in_=t[rows, 0, :])
+            hn_rows = two.tile([P, FEATURES], F32, name="hn_rows")
+            nc.sync.dma_start(out=hn_rows[:], in_=hn[0, rows, :])
+            loaded[i] = {"x": x_rows, "gates": gate_rows, "grad": grad_rows, "t": t_rows, "hn": hn_rows}
+
+        def prepare(i):
+            rows = loaded[i]
+            neg_x = two.tile([P, FEATURES], F32, name="neg_x")
+            nc.scalar.mul(neg_x[:], rows["x"][:], -1.0)
+            grad_t = two.tile([P, FEATURES], F32, name="grad_t")
+            nc.gpsimd.tensor_tensor(out=grad_t[:], in0=rows["grad"][:], in1=rows["t"][:], op=ALU.mult)
+            c_squared = []
+            r_factor = []
+            for d in range(DIRECTIONS):
+                c_sq = six.tile([P, FEATURES], F32, name="c_squared")
+                nc.scalar.square(c_sq[:], rows["gates"][d][:, C_COLS])
+                c_squared.append(c_sq)
+                factor = six.tile([P, FEATURES], F32, name="r_factor")
+                nc.scalar.activation(
+                    out=factor[:], in_=rows["gates"][d][:, R_COLS], func=FUNC.Copy, scale=-1.0, bias=1.0
+                )
+                r_factor.append(factor)
+            for d in range(DIRECTIONS):
+                nc.gpsimd.tensor_tensor(
+                    out=r_factor[d][:], in0=r_factor[d][:], in1=rows["gates"][d][:, R_COLS], op=ALU.mult
+                )
+            for d in range(DIRECTIONS):
+                nc.gpsimd.tensor_tensor(
+                    out=r_factor[d][:], in0=r_factor[d][:], in1=rows["hn"][:], op=ALU.mult
+                )
+            prepared[i] = {"neg_x": neg_x, "grad_t": grad_t, "c_squared": c_squared, "r_factor": r_factor}
+
+        def transposed_sum(bank_name, terms):
+            bank = psum.tile([P, CHUNKS, P], F32, name=bank_name)
+            for chunk in range(CHUNKS):
+                cols = slice(chunk * P, (chunk + 1) * P)
+                for k, term in enumerate(terms):
+                    nc.tensor.matmul(
+                        bank[:, chunk, :],
+                        lhsT=term[:, cols],
+                        rhs=identity[:],
+                        is_transpose=True,
+                        start=(k == 0),
+                        stop=(k == len(terms) - 1),
+                    )
+            return bank
+
+        def fill_ec(i, d):
+            c_rows = loaded[i]["gates"][d][:, C_COLS]
+            bank = transposed_sum("a%d" % d, [c_rows, prepared[i]["neg_x"][:]])
+            ec = three.tile([P, P, CHUNKS], F32, name="ec")
+            nc.scalar.copy(out=ec[:], in_=by_node(bank))
+            state[i]["ec"].append(ec)
+
+        def fill_grad_t(i):
+            banks["grad_t"] = transposed_sum("a0", [prepared[i]["grad_t"][:]])
+
+        def fill_c_squared(i, d):
+            banks["c_squared", d] = transposed_sum("a%d" % (d + 1), [prepared[i]["c_squared"][d][:]])
+
+        def fill_c_sum(i):
+            banks["c_sum"] = transposed_sum("a3", [rzc[:, C_COLS] for rzc in loaded[i]["gates"]])
+
+        def fill_z(i, d):
+            banks["z", d] = transposed_sum("b%d" % d, [loaded[i]["gates"][d][:, Z_COLS]])
+
+        def fill_r_factor(i, d):
+            banks["r_factor", d] = transposed_sum("b%d" % d, [prepared[i]["r_factor"][d][:]])
+
+        def new_state(i):
+            state[i] = {"ec": [], "zec": [], "p": [], "dr": [], "dz": [], "dc": []}
+
+        def quantise_weights():
+            w_rows = once.tile([P, GATES, CHUNKS, FEATURES], BF16, name="w_rows")
+            nc.sync.dma_start(
+                out=w_rows[:], in_=wih.rearrange("(g t p) n -> p g t n", t=CHUNKS, p=P)
+            )
+            w_grouped = once.tile([P, GATES, FEATURES, CHUNKS], BF16, name="w_grouped", align_bytes=64)
+            w_codes = once.tile([P, GATES, FEATURES], U32, name="w_codes", align_bytes=64)
+            w_scales = once.tile([P, GATES, FEATURES], U8, name="w_scales", align_bytes=64)
+            for g in range(GATES):
+                nc.scalar.copy(out=w_grouped[:, g], in_=w_rows[:, g].rearrange("p t n -> p n t"))
+            for g in range(GATES):
+                nc.vector.quantize_mx(
+                    out=w_codes[:, g, :].bitcast(E4M3_X4),
+                    scales=w_scales[:, g, :],
+                    in_=w_grouped[:, g].rearrange("p n t -> p (n t)"),
+                )
+            return w_codes, w_scales
+
+        def gate_z_gradient(i):
+            for d in range(DIRECTIONS):
+                dz = three.tile([P, P, CHUNKS], BF16, name="dz", align_bytes=64)
+                nc.vector.tensor_tensor(
+                    out=dz[:], in0=state[i]["p"][d][:], in1=state[i]["zec"][d][:], op=ALU.mult
+                )
+                state[i]["dz"].append(dz)
+
+        def quantise(i):
+            codes = two.tile([P, DIRECTIONS, GATES, P], U32, name="codes", align_bytes=64)
+            scales = two.tile([P, DIRECTIONS, GATES, P], U8, name="scales", align_bytes=64)
+            for d in range(DIRECTIONS):
+                for g, kind in enumerate(("dr", "dz", "dc")):
+                    nc.vector.quantize_mx(
+                        out=codes[:, d, g, :].bitcast(E5M2_X4),
+                        scales=scales[:, d, g, :],
+                        in_=state[i][kind][d][:].rearrange("p n t -> p (n t)"),
+                    )
+            state[i]["codes"] = codes
+            state[i]["scales"] = scales
+
+        def multiply(i, w_codes, w_scales):
+            rows = slice(i * P, (i + 1) * P)
+            for d in range(DIRECTIONS):
+                acc = psum.tile([P, FEATURES], F32, name="acc")
+                for g in range(GATES):
+                    nc.tensor.matmul_mx(
+                        out=acc[:],
+                        lhsT=state[i]["codes"][:, d, g, :].bitcast(E5M2_X4),
+                        lhsT_scale=state[i]["scales"][:, d, g, :],
+                        rhs=w_codes[:, g, :].bitcast(E4M3_X4),
+                        rhs_scale=w_scales[:, g, :],
+                        start=(g == 0),
+                        stop=(g == GATES - 1),
+                    )
+                result = three.tile([P, FEATURES], F32, name="result")
+                nc.scalar.copy(out=result[:], in_=acc[:])
+                nc.scalar.dma_start(out=out[d, 0, rows, :], in_=result[:])
+
+        def gradient(i, w_codes, w_scales):
+            following = i + 1
+            if i + 2 < NODE_TILES:
+                load(i + 2)
+            if following < NODE_TILES:
+                prepare(following)
+                new_state(following)
+            mine = state[i]
+
+            for d in range(DIRECTIONS):
+                zec = six.tile([P, P, CHUNKS], F32, name="zec")
+                nc.vector.tensor_tensor(out=zec[:], in0=by_node(banks["z", d]), in1=mine["ec"][d][:], op=ALU.mult)
+                mine["zec"].append(zec)
+
+            if i >= 2:
+                multiply(i - 2, w_codes, w_scales)
+
+            zec_sum = two.tile([P, P, CHUNKS], F32, name="zec_sum")
+            nc.vector.tensor_tensor(out=zec_sum[:], in0=mine["zec"][0][:], in1=mine["zec"][1][:], op=ALU.add)
+            if i >= 1:
+                gate_z_gradient(i - 1)
+            nc.vector.tensor_tensor(out=zec_sum[:], in0=zec_sum[:], in1=mine["zec"][2][:], op=ALU.add)
+            if i >= 1:
+                quantise(i - 1)
+
+            positive = two.tile([P, P, CHUNKS], F32, name="positive")
+            nc.vector.tensor_tensor(out=positive[:], in0=by_node(banks["c_sum"]), in1=zec_sum[:], op=ALU.is_gt)
+            fill_c_squared(i, 2)
+            ds = two.tile([P, P, CHUNKS], F32, name="ds")
+            nc.vector.tensor_tensor(out=ds[:], in0=by_node(banks["grad_t"]), in1=positive[:], op=ALU.mult)
+            if following < NODE_TILES:
+                fill_ec(following, 0)
+                fill_grad_t(following)
+
+            for d in range(DIRECTIONS):
+                p = three.tile([P, P, CHUNKS], F32, name="p")
+                nc.vector.scalar_tensor_tensor(
+                    out=p[:], in0=by_node(banks["z", d]), scalar=1.0, in1=ds[:], op0=ALU.subtract, op1=ALU.mult
+                )
+                mine["p"].append(p)
+                fill_r_factor(i, d)
+
+            dc_f32 = []
+            for d in range(DIRECTIONS):
+                dc_exact = three.tile([P, P, CHUNKS], F32, name="dc_exact")
+                nc.vector.scalar_tensor_tensor(
+                    out=dc_exact[:],
+                    in0=by_node(banks["c_squared", d]),
+                    scalar=1.0,
+                    in1=mine["p"][d][:],
+                    op0=ALU.subtract,
+                    op1=ALU.mult,
+                )
+                dc_f32.append(dc_exact)
+                dc = three.tile([P, P, CHUNKS], BF16, name="dc", align_bytes=64)
+                nc.scalar.copy(out=dc[:], in_=dc_exact[:])
+                mine["dc"].append(dc)
+                if following < NODE_TILES and d + 1 < DIRECTIONS:
+                    fill_ec(following, d + 1)
+
+            for d in range(DIRECTIONS):
+                dr = three.tile([P, P, CHUNKS], BF16, name="dr", align_bytes=64)
+                nc.vector.tensor_tensor(out=dr[:], in0=by_node(banks["r_factor", d]), in1=dc_f32[d][:], op=ALU.mult)
+                mine["dr"].append(dr)
+                if following < NODE_TILES:
+                    fill_z(following, d)
+
+            if following < NODE_TILES:
+                fill_c_sum(following)
+                fill_c_squared(following, 0)
+                fill_c_squared(following, 1)
+
+        load(0)
+        load(1)
+        prepare(0)
+        new_state(0)
+        for d in range(DIRECTIONS):
+            fill_ec(0, d)
+            fill_z(0, d)
+        fill_c_sum(0)
+        fill_grad_t(0)
+        fill_c_squared(0, 0)
+        fill_c_squared(0, 1)
+        w_codes, w_scales = quantise_weights()
+
+        for i in range(NODE_TILES):
+            gradient(i, w_codes, w_scales)
+
+        gate_z_gradient(NODE_TILES - 1)
+        quantise(NODE_TILES - 1)
+        multiply(NODE_TILES - 2, w_codes, w_scales)
+        multiply(NODE_TILES - 1, w_codes, w_scales)

@@ -48,9 +48,12 @@ def tile_graphconvolution_pb_v_kernel(
         three = ctx.enter_context(tc.tile_pool(name="three", bufs=DIRECTIONS))
         six = ctx.enter_context(tc.tile_pool(name="six", bufs=2 * DIRECTIONS))
         psum = ctx.enter_context(tc.psum_pool(name="psum", bufs=1))
+        psum_pair = ctx.enter_context(tc.psum_pool(name="psum_pair", bufs=2))
 
         identity = once.tile([P, P], F32, name="identity")
         make_identity(nc, identity[:])
+        identity_bf16 = once.tile([P, P], BF16, name="identity_bf16")
+        make_identity(nc, identity_bf16[:])
 
         loaded = {}
         prepared = {}
@@ -59,87 +62,78 @@ def tile_graphconvolution_pb_v_kernel(
 
         def load(i):
             rows = slice(i * P, (i + 1) * P)
-            x_rows = two.tile([P, FEATURES], BF16, name="x_rows")
-            nc.sync.dma_start(out=x_rows[:], in_=x[rows, 0, :])
-            gate_rows = []
-            for d in range(DIRECTIONS):
-                rzc = six.tile([P, GATES * FEATURES], F32, name="gate_rows")
-                nc.sync.dma_start(out=rzc[:], in_=gates[d, 0, rows, :])
-                gate_rows.append(rzc)
-            grad_rows = two.tile([P, FEATURES], BF16, name="grad_rows")
-            nc.sync.dma_start(out=grad_rows[:], in_=grad_out[rows, 0, :])
-            t_rows = two.tile([P, FEATURES], F32, name="t_rows")
-            nc.sync.dma_start(out=t_rows[:], in_=t[rows, 0, :])
-            hn_rows = two.tile([P, FEATURES], F32, name="hn_rows")
-            nc.sync.dma_start(out=hn_rows[:], in_=hn[0, rows, :])
-            loaded[i] = {"x": x_rows, "gates": gate_rows, "grad": grad_rows, "t": t_rows, "hn": hn_rows}
+            tiles = {}
+
+            def fetch(name, shape, dtype, source):
+                tiles[name] = two.tile(shape, dtype, name=name + "_rows")
+                nc.sync.dma_start(out=tiles[name][:], in_=source)
+
+            def gate(cols):
+                return gates[:, 0, rows, cols].rearrange("d n k -> n d k")
+
+            fetch("x", [P, FEATURES], BF16, x[rows, 0, :])
+            fetch("c", [P, DIRECTIONS, FEATURES], F32, gate(C_COLS))
+            fetch("z", [P, DIRECTIONS, FEATURES], F32, gate(Z_COLS))
+            fetch("grad", [P, FEATURES], BF16, grad_out[rows, 0, :])
+            fetch("t", [P, FEATURES], F32, t[rows, 0, :])
+            fetch("r", [P, DIRECTIONS, FEATURES], F32, gate(R_COLS))
+            fetch("hn", [P, FEATURES], F32, hn[0, rows, :])
+            loaded[i] = tiles
+            state[i] = {"zec": [], "p": [], "dr": [], "dz": [], "dc": []}
 
         def prepare(i):
             rows = loaded[i]
-            neg_x = two.tile([P, FEATURES], F32, name="neg_x")
-            nc.scalar.mul(neg_x[:], rows["x"][:], -1.0)
             grad_t = two.tile([P, FEATURES], F32, name="grad_t")
             nc.gpsimd.tensor_tensor(out=grad_t[:], in0=rows["grad"][:], in1=rows["t"][:], op=ALU.mult)
             c_squared = []
             r_factor = []
             for d in range(DIRECTIONS):
                 c_sq = six.tile([P, FEATURES], F32, name="c_squared")
-                nc.scalar.square(c_sq[:], rows["gates"][d][:, C_COLS])
+                nc.scalar.square(c_sq[:], rows["c"][:, d, :])
                 c_squared.append(c_sq)
+            for d in range(DIRECTIONS):
                 factor = six.tile([P, FEATURES], F32, name="r_factor")
                 nc.scalar.activation(
-                    out=factor[:], in_=rows["gates"][d][:, R_COLS], func=FUNC.Copy, scale=-1.0, bias=1.0
+                    out=factor[:], in_=rows["r"][:, d, :], func=FUNC.Square, bias=-0.5, scale=1.0
                 )
                 r_factor.append(factor)
             for d in range(DIRECTIONS):
-                nc.gpsimd.tensor_tensor(
-                    out=r_factor[d][:], in0=r_factor[d][:], in1=rows["gates"][d][:, R_COLS], op=ALU.mult
-                )
-            for d in range(DIRECTIONS):
+                nc.scalar.activation(out=r_factor[d][:], in_=r_factor[d][:], func=FUNC.Copy, scale=-1.0, bias=0.25)
                 nc.gpsimd.tensor_tensor(
                     out=r_factor[d][:], in0=r_factor[d][:], in1=rows["hn"][:], op=ALU.mult
                 )
-            prepared[i] = {"neg_x": neg_x, "grad_t": grad_t, "c_squared": c_squared, "r_factor": r_factor}
+            prepared[i] = {"grad_t": grad_t, "c_squared": c_squared, "r_factor": r_factor}
 
-        def transposed_sum(bank_name, terms):
+        def transposed(bank_name, rows):
             bank = psum.tile([P, CHUNKS, P], F32, name=bank_name)
             for chunk in range(CHUNKS):
-                cols = slice(chunk * P, (chunk + 1) * P)
-                for k, term in enumerate(terms):
-                    nc.tensor.matmul(
-                        bank[:, chunk, :],
-                        lhsT=term[:, cols],
-                        rhs=identity[:],
-                        is_transpose=True,
-                        start=(k == 0),
-                        stop=(k == len(terms) - 1),
-                    )
+                nc.tensor.transpose(bank[:, chunk, :], rows[:, chunk * P : (chunk + 1) * P], identity[:])
             return bank
 
-        def fill_ec(i, d):
-            c_rows = loaded[i]["gates"][d][:, C_COLS]
-            bank = transposed_sum("a%d" % d, [c_rows, prepared[i]["neg_x"][:]])
-            ec = three.tile([P, P, CHUNKS], F32, name="ec")
-            nc.scalar.copy(out=ec[:], in_=by_node(bank))
-            state[i]["ec"].append(ec)
+        def fill_c(i, d):
+            banks["c", d] = transposed("a%d" % d, loaded[i]["c"][:, d, :])
 
         def fill_grad_t(i):
-            banks["grad_t"] = transposed_sum("a0", [prepared[i]["grad_t"][:]])
+            banks["grad_t"] = transposed("a0", prepared[i]["grad_t"][:])
 
         def fill_c_squared(i, d):
-            banks["c_squared", d] = transposed_sum("a%d" % (d + 1), [prepared[i]["c_squared"][d][:]])
-
-        def fill_c_sum(i):
-            banks["c_sum"] = transposed_sum("a3", [rzc[:, C_COLS] for rzc in loaded[i]["gates"]])
+            banks["c_squared", d] = transposed("a%d" % d, prepared[i]["c_squared"][d][:])
 
         def fill_z(i, d):
-            banks["z", d] = transposed_sum("b%d" % d, [loaded[i]["gates"][d][:, Z_COLS]])
+            banks["z", d] = transposed("b%d" % d, loaded[i]["z"][:, d, :])
 
         def fill_r_factor(i, d):
-            banks["r_factor", d] = transposed_sum("b%d" % d, [prepared[i]["r_factor"][d][:]])
+            banks["r_factor", d] = transposed("b%d" % d, prepared[i]["r_factor"][d][:])
 
-        def new_state(i):
-            state[i] = {"ec": [], "zec": [], "p": [], "dr": [], "dz": [], "dc": []}
+        def turn_h(i):
+            bank = psum_pair.tile([P, CHUNKS, P], BF16, name="pair")
+            for chunk in range(CHUNKS):
+                nc.tensor.transpose(
+                    bank[:, chunk, :], loaded[i]["x"][:, chunk * P : (chunk + 1) * P], identity_bf16[:]
+                )
+            h = two.tile([P, P, CHUNKS], BF16, name="h")
+            nc.scalar.copy(out=h[:], in_=by_node(bank))
+            state[i]["h"] = h
 
         def quantise_weights():
             w_rows = once.tile([P, GATES, CHUNKS, FEATURES], BF16, name="w_rows")
@@ -159,14 +153,6 @@ def tile_graphconvolution_pb_v_kernel(
                 )
             return w_codes, w_scales
 
-        def gate_z_gradient(i):
-            for d in range(DIRECTIONS):
-                dz = three.tile([P, P, CHUNKS], BF16, name="dz", align_bytes=64)
-                nc.vector.tensor_tensor(
-                    out=dz[:], in0=state[i]["p"][d][:], in1=state[i]["zec"][d][:], op=ALU.mult
-                )
-                state[i]["dz"].append(dz)
-
         def quantise(i):
             codes = two.tile([P, DIRECTIONS, GATES, P], U32, name="codes", align_bytes=64)
             scales = two.tile([P, DIRECTIONS, GATES, P], U8, name="scales", align_bytes=64)
@@ -183,7 +169,7 @@ def tile_graphconvolution_pb_v_kernel(
         def multiply(i, w_codes, w_scales):
             rows = slice(i * P, (i + 1) * P)
             for d in range(DIRECTIONS):
-                acc = psum.tile([P, FEATURES], F32, name="acc")
+                acc = psum_pair.tile([P, FEATURES], F32, name="pair")
                 for g in range(GATES):
                     nc.tensor.matmul_mx(
                         out=acc[:],
@@ -204,33 +190,38 @@ def tile_graphconvolution_pb_v_kernel(
                 load(i + 2)
             if following < NODE_TILES:
                 prepare(following)
-                new_state(following)
             mine = state[i]
 
+            ec = []
+            for d in range(DIRECTIONS):
+                difference = three.tile([P, P, CHUNKS], F32, name="ec")
+                nc.vector.tensor_tensor(out=difference[:], in0=by_node(banks["c", d]), in1=mine["h"][:], op=ALU.subtract)
+                ec.append(difference)
             for d in range(DIRECTIONS):
                 zec = six.tile([P, P, CHUNKS], F32, name="zec")
-                nc.vector.tensor_tensor(out=zec[:], in0=by_node(banks["z", d]), in1=mine["ec"][d][:], op=ALU.mult)
+                nc.vector.tensor_tensor(out=zec[:], in0=by_node(banks["z", d]), in1=ec[d][:], op=ALU.mult)
                 mine["zec"].append(zec)
+            h_new = []
+            for d in range(DIRECTIONS):
+                blend = three.tile([P, P, CHUNKS], F32, name="h_new")
+                nc.vector.tensor_tensor(out=blend[:], in0=by_node(banks["c", d]), in1=mine["zec"][d][:], op=ALU.subtract)
+                h_new.append(blend)
+                if d == 0:
+                    fill_grad_t(i)
+                else:
+                    fill_c_squared(i, d)
 
-            if i >= 2:
-                multiply(i - 2, w_codes, w_scales)
-
-            zec_sum = two.tile([P, P, CHUNKS], F32, name="zec_sum")
-            nc.vector.tensor_tensor(out=zec_sum[:], in0=mine["zec"][0][:], in1=mine["zec"][1][:], op=ALU.add)
-            if i >= 1:
-                gate_z_gradient(i - 1)
-            nc.vector.tensor_tensor(out=zec_sum[:], in0=zec_sum[:], in1=mine["zec"][2][:], op=ALU.add)
+            hsum = two.tile([P, P, CHUNKS], F32, name="hsum")
+            nc.vector.tensor_tensor(out=hsum[:], in0=h_new[0][:], in1=h_new[1][:], op=ALU.add)
+            nc.vector.tensor_tensor(out=hsum[:], in0=hsum[:], in1=h_new[2][:], op=ALU.add)
             if i >= 1:
                 quantise(i - 1)
 
-            positive = two.tile([P, P, CHUNKS], F32, name="positive")
-            nc.vector.tensor_tensor(out=positive[:], in0=by_node(banks["c_sum"]), in1=zec_sum[:], op=ALU.is_gt)
-            fill_c_squared(i, 2)
             ds = two.tile([P, P, CHUNKS], F32, name="ds")
-            nc.vector.tensor_tensor(out=ds[:], in0=by_node(banks["grad_t"]), in1=positive[:], op=ALU.mult)
-            if following < NODE_TILES:
-                fill_ec(following, 0)
-                fill_grad_t(following)
+            nc.vector.scalar_tensor_tensor(
+                out=ds[:], in0=hsum[:], scalar=0.0, in1=by_node(banks["grad_t"]), op0=ALU.is_gt, op1=ALU.mult
+            )
+            fill_c_squared(i, 0)
 
             for d in range(DIRECTIONS):
                 p = three.tile([P, P, CHUNKS], F32, name="p")
@@ -239,6 +230,14 @@ def tile_graphconvolution_pb_v_kernel(
                 )
                 mine["p"].append(p)
                 fill_r_factor(i, d)
+                dz = three.tile([P, P, CHUNKS], BF16, name="dz", align_bytes=64)
+                nc.gpsimd.tensor_tensor(out=dz[:], in0=p[:], in1=mine["zec"][d][:], op=ALU.mult)
+                mine["dz"].append(dz)
+
+            if i >= 1:
+                multiply(i - 1, w_codes, w_scales)
+            if following < NODE_TILES:
+                turn_h(following)
 
             dc_f32 = []
             for d in range(DIRECTIONS):
@@ -255,8 +254,8 @@ def tile_graphconvolution_pb_v_kernel(
                 dc = three.tile([P, P, CHUNKS], BF16, name="dc", align_bytes=64)
                 nc.scalar.copy(out=dc[:], in_=dc_exact[:])
                 mine["dc"].append(dc)
-                if following < NODE_TILES and d + 1 < DIRECTIONS:
-                    fill_ec(following, d + 1)
+                if following < NODE_TILES:
+                    fill_c(following, d)
 
             for d in range(DIRECTIONS):
                 dr = three.tile([P, P, CHUNKS], BF16, name="dr", align_bytes=64)
@@ -265,28 +264,18 @@ def tile_graphconvolution_pb_v_kernel(
                 if following < NODE_TILES:
                     fill_z(following, d)
 
-            if following < NODE_TILES:
-                fill_c_sum(following)
-                fill_c_squared(following, 0)
-                fill_c_squared(following, 1)
-
         load(0)
-        load(1)
-        prepare(0)
-        new_state(0)
+        turn_h(0)
         for d in range(DIRECTIONS):
-            fill_ec(0, d)
+            fill_c(0, d)
+        for d in range(DIRECTIONS):
             fill_z(0, d)
-        fill_c_sum(0)
-        fill_grad_t(0)
-        fill_c_squared(0, 0)
-        fill_c_squared(0, 1)
+        prepare(0)
+        load(1)
         w_codes, w_scales = quantise_weights()
 
         for i in range(NODE_TILES):
             gradient(i, w_codes, w_scales)
 
-        gate_z_gradient(NODE_TILES - 1)
         quantise(NODE_TILES - 1)
-        multiply(NODE_TILES - 2, w_codes, w_scales)
         multiply(NODE_TILES - 1, w_codes, w_scales)

@@ -135,38 +135,41 @@ def tile_graphconvolution_pb_v_kernel(
             nc.scalar.copy(out=h[:], in_=by_node(bank))
             state[i]["h"] = h
 
-        def quantise_weights():
-            w_rows = once.tile([P, GATES, CHUNKS, FEATURES], BF16, name="w_rows")
+        w_rows = once.tile([P, GATES, CHUNKS, FEATURES], BF16, name="w_rows")
+
+        def load_weights():
             nc.sync.dma_start(
                 out=w_rows[:], in_=wih.rearrange("(g t p) n -> p g t n", t=CHUNKS, p=P)
             )
-            w_grouped = once.tile([P, GATES, FEATURES, CHUNKS], BF16, name="w_grouped", align_bytes=64)
-            w_codes = once.tile([P, GATES, FEATURES], U32, name="w_codes", align_bytes=64)
-            w_scales = once.tile([P, GATES, FEATURES], U8, name="w_scales", align_bytes=64)
+
+        w_grouped = once.tile([P, GATES, FEATURES, CHUNKS], BF16, name="w_grouped", align_bytes=64)
+        w_codes = once.tile([P, GATES, FEATURES], U32, name="w_codes", align_bytes=64)
+        w_scales = once.tile([P, GATES, FEATURES], U8, name="w_scales", align_bytes=64)
+
+        def regroup_weights():
             for g in range(GATES):
                 nc.scalar.copy(out=w_grouped[:, g], in_=w_rows[:, g].rearrange("p t n -> p n t"))
+
+        def quantise_weights():
             for g in range(GATES):
                 nc.vector.quantize_mx(
                     out=w_codes[:, g, :].bitcast(E4M3_X4),
                     scales=w_scales[:, g, :],
                     in_=w_grouped[:, g].rearrange("p n t -> p (n t)"),
                 )
-            return w_codes, w_scales
 
-        def quantise(i):
-            codes = two.tile([P, DIRECTIONS, GATES, P], U32, name="codes", align_bytes=64)
-            scales = two.tile([P, DIRECTIONS, GATES, P], U8, name="scales", align_bytes=64)
-            for d in range(DIRECTIONS):
-                for g, kind in enumerate(("dr", "dz", "dc")):
-                    nc.vector.quantize_mx(
-                        out=codes[:, d, g, :].bitcast(E5M2_X4),
-                        scales=scales[:, d, g, :],
-                        in_=state[i][kind][d][:].rearrange("p n t -> p (n t)"),
-                    )
-            state[i]["codes"] = codes
-            state[i]["scales"] = scales
+        def quantise(i, d):
+            if d == 0:
+                state[i]["codes"] = two.tile([P, DIRECTIONS, GATES, P], U32, name="codes", align_bytes=64)
+                state[i]["scales"] = two.tile([P, DIRECTIONS, GATES, P], U8, name="scales", align_bytes=64)
+            for g, kind in enumerate(("dr", "dz", "dc")):
+                nc.vector.quantize_mx(
+                    out=state[i]["codes"][:, d, g, :].bitcast(E5M2_X4),
+                    scales=state[i]["scales"][:, d, g, :],
+                    in_=state[i][kind][d][:].rearrange("p n t -> p (n t)"),
+                )
 
-        def multiply(i, w_codes, w_scales):
+        def multiply(i):
             rows = slice(i * P, (i + 1) * P)
             for d in range(DIRECTIONS):
                 acc = psum_pair.tile([P, FEATURES], F32, name="pair")
@@ -184,8 +187,10 @@ def tile_graphconvolution_pb_v_kernel(
                 nc.scalar.copy(out=result[:], in_=acc[:])
                 nc.scalar.dma_start(out=out[d, 0, rows, :], in_=result[:])
 
-        def gradient(i, w_codes, w_scales):
+        def gradient(i):
             following = i + 1
+            if i >= 2:
+                multiply(i - 2)
             if i + 2 < NODE_TILES:
                 load(i + 2)
             if following < NODE_TILES:
@@ -213,9 +218,12 @@ def tile_graphconvolution_pb_v_kernel(
 
             hsum = two.tile([P, P, CHUNKS], F32, name="hsum")
             nc.vector.tensor_tensor(out=hsum[:], in0=h_new[0][:], in1=h_new[1][:], op=ALU.add)
+            if i >= 1:
+                quantise(i - 1, 0)
             nc.vector.tensor_tensor(out=hsum[:], in0=hsum[:], in1=h_new[2][:], op=ALU.add)
             if i >= 1:
-                quantise(i - 1)
+                quantise(i - 1, 1)
+                quantise(i - 1, 2)
 
             ds = two.tile([P, P, CHUNKS], F32, name="ds")
             nc.vector.scalar_tensor_tensor(
@@ -234,8 +242,6 @@ def tile_graphconvolution_pb_v_kernel(
                 nc.gpsimd.tensor_tensor(out=dz[:], in0=p[:], in1=mine["zec"][d][:], op=ALU.mult)
                 mine["dz"].append(dz)
 
-            if i >= 1:
-                multiply(i - 1, w_codes, w_scales)
             if following < NODE_TILES:
                 turn_h(following)
 
@@ -264,6 +270,8 @@ def tile_graphconvolution_pb_v_kernel(
                 if following < NODE_TILES:
                     fill_z(following, d)
 
+        ctx.enter_context(tc.manual_schedule())
+
         load(0)
         turn_h(0)
         for d in range(DIRECTIONS):
@@ -272,10 +280,16 @@ def tile_graphconvolution_pb_v_kernel(
             fill_z(0, d)
         prepare(0)
         load(1)
-        w_codes, w_scales = quantise_weights()
+        load_weights()
 
-        for i in range(NODE_TILES):
-            gradient(i, w_codes, w_scales)
+        gradient(0)
+        regroup_weights()
+        gradient(1)
+        quantise_weights()
+        for i in range(2, NODE_TILES):
+            gradient(i)
 
-        quantise(NODE_TILES - 1)
-        multiply(NODE_TILES - 1, w_codes, w_scales)
+        multiply(NODE_TILES - 2)
+        for d in range(DIRECTIONS):
+            quantise(NODE_TILES - 1, d)
+        multiply(NODE_TILES - 1)

@@ -19,6 +19,7 @@ FEATURES = 512
 GATES = 3
 CHUNKS = FEATURES // P
 NODE_TILES = NODES // P
+OPERANDS = DIRECTIONS * GATES
 
 R_COLS = slice(0, FEATURES)
 Z_COLS = slice(FEATURES, 2 * FEATURES)
@@ -79,42 +80,54 @@ def tile_graphconvolution_pb_v_kernel(
             fetch("r", [P, DIRECTIONS, FEATURES], F32, gate(R_COLS))
             fetch("hn", [P, FEATURES], F32, hn[0, rows, :])
             loaded[i] = tiles
-            state[i] = {"zec": [], "p": [], "dr": [], "dz": [], "dc": []}
+            prepared[i] = {"c_squared": [], "r_factor": []}
+            state[i] = {"zec": [], "p": []}
 
-        def prepare(i):
+        def prepare_squares(i):
             rows = loaded[i]
             grad_t = two.tile([P, FEATURES], F32, name="grad_t")
             nc.gpsimd.tensor_tensor(out=grad_t[:], in0=rows["grad"][:], in1=rows["t"][:], op=ALU.mult)
-            c_squared = []
-            r_factor = []
+            prepared[i]["grad_t"] = grad_t
             for d in range(DIRECTIONS):
                 c_sq = six.tile([P, FEATURES], F32, name="c_squared")
                 nc.scalar.square(c_sq[:], rows["c"][:, d, :])
-                c_squared.append(c_sq)
+                prepared[i]["c_squared"].append(c_sq)
             for d in range(DIRECTIONS):
                 factor = six.tile([P, FEATURES], F32, name="r_factor")
-                nc.scalar.activation(
-                    out=factor[:], in_=rows["r"][:, d, :], func=FUNC.Square, bias=-0.5, scale=1.0
-                )
-                r_factor.append(factor)
-            for d in range(DIRECTIONS):
-                nc.scalar.activation(out=r_factor[d][:], in_=r_factor[d][:], func=FUNC.Copy, scale=-1.0, bias=0.25)
-                nc.gpsimd.tensor_tensor(
-                    out=r_factor[d][:], in0=r_factor[d][:], in1=rows["hn"][:], op=ALU.mult
-                )
-            prepared[i] = {"grad_t": grad_t, "c_squared": c_squared, "r_factor": r_factor}
+                nc.scalar.activation(out=factor[:], in_=rows["r"][:, d, :], func=FUNC.Square, bias=-0.5, scale=1.0)
+                prepared[i]["r_factor"].append(factor)
+
+        def prepare_r_factor(i):
+            for factor in prepared[i]["r_factor"]:
+                nc.scalar.activation(out=factor[:], in_=factor[:], func=FUNC.Copy, scale=-1.0, bias=0.25)
+                nc.gpsimd.tensor_tensor(out=factor[:], in0=factor[:], in1=loaded[i]["hn"][:], op=ALU.mult)
 
         def transposed(bank_name, rows):
             bank = psum.tile([P, CHUNKS, P], F32, name=bank_name)
-            for chunk in range(CHUNKS):
+            nc.tensor.matmul(bank[:, 0, :], lhsT=rows[:, 0:P], rhs=identity[:], start=True, stop=True)
+            for chunk in range(1, CHUNKS):
                 nc.tensor.transpose(bank[:, chunk, :], rows[:, chunk * P : (chunk + 1) * P], identity[:])
             return bank
 
         def fill_c(i, d):
             banks["c", d] = transposed("a%d" % d, loaded[i]["c"][:, d, :])
 
+        def fill_c_sum(i):
+            bank = psum.tile([P, CHUNKS, P], F32, name="a0")
+            for chunk in range(CHUNKS):
+                for d in range(DIRECTIONS):
+                    nc.tensor.matmul(
+                        bank[:, chunk, :],
+                        lhsT=loaded[i]["c"][:, d, chunk * P : (chunk + 1) * P],
+                        rhs=identity[:],
+                        is_transpose=True,
+                        start=(d == 0),
+                        stop=(d == DIRECTIONS - 1),
+                    )
+            banks["c_sum"] = bank
+
         def fill_grad_t(i):
-            banks["grad_t"] = transposed("a0", prepared[i]["grad_t"][:])
+            banks["grad_t"] = transposed("a1", prepared[i]["grad_t"][:])
 
         def fill_c_squared(i, d):
             banks["c_squared", d] = transposed("a%d" % d, prepared[i]["c_squared"][d][:])
@@ -136,15 +149,14 @@ def tile_graphconvolution_pb_v_kernel(
             state[i]["h"] = h
 
         w_rows = once.tile([P, GATES, CHUNKS, FEATURES], BF16, name="w_rows")
+        w_grouped = once.tile([P, GATES, FEATURES, CHUNKS], BF16, name="w_grouped", align_bytes=64)
+        w_codes = once.tile([P, GATES, FEATURES], U32, name="w_codes", align_bytes=64)
+        w_scales = once.tile([P, GATES, FEATURES], U8, name="w_scales", align_bytes=64)
 
         def load_weights():
             nc.sync.dma_start(
                 out=w_rows[:], in_=wih.rearrange("(g t p) n -> p g t n", t=CHUNKS, p=P)
             )
-
-        w_grouped = once.tile([P, GATES, FEATURES, CHUNKS], BF16, name="w_grouped", align_bytes=64)
-        w_codes = once.tile([P, GATES, FEATURES], U32, name="w_codes", align_bytes=64)
-        w_scales = once.tile([P, GATES, FEATURES], U8, name="w_scales", align_bytes=64)
 
         def regroup_weights():
             for g in range(GATES):
@@ -158,16 +170,16 @@ def tile_graphconvolution_pb_v_kernel(
                     in_=w_grouped[:, g].rearrange("p n t -> p (n t)"),
                 )
 
-        def quantise(i, d):
-            if d == 0:
-                state[i]["codes"] = two.tile([P, DIRECTIONS, GATES, P], U32, name="codes", align_bytes=64)
-                state[i]["scales"] = two.tile([P, DIRECTIONS, GATES, P], U8, name="scales", align_bytes=64)
-            for g, kind in enumerate(("dr", "dz", "dc")):
-                nc.vector.quantize_mx(
-                    out=state[i]["codes"][:, d, g, :].bitcast(E5M2_X4),
-                    scales=state[i]["scales"][:, d, g, :],
-                    in_=state[i][kind][d][:].rearrange("p n t -> p (n t)"),
-                )
+        def quantise(i, first, count):
+            if first == 0:
+                state[i]["codes"] = two.tile([P, OPERANDS, P], U32, name="codes", align_bytes=64)
+                state[i]["scales"] = two.tile([P, OPERANDS, P], U8, name="scales", align_bytes=64)
+            some = slice(first, first + count)
+            nc.vector.quantize_mx(
+                out=state[i]["codes"][:, some, :].rearrange("p u n -> p (u n)").bitcast(E5M2_X4),
+                scales=state[i]["scales"][:, some, :].rearrange("p u n -> p (u n)"),
+                in_=state[i]["dgi"][:, some].rearrange("p u n t -> p (u n t)"),
+            )
 
         def multiply(i):
             rows = slice(i * P, (i + 1) * P)
@@ -176,8 +188,8 @@ def tile_graphconvolution_pb_v_kernel(
                 for g in range(GATES):
                     nc.tensor.matmul_mx(
                         out=acc[:],
-                        lhsT=state[i]["codes"][:, d, g, :].bitcast(E5M2_X4),
-                        lhsT_scale=state[i]["scales"][:, d, g, :],
+                        lhsT=state[i]["codes"][:, GATES * d + g, :].bitcast(E5M2_X4),
+                        lhsT_scale=state[i]["scales"][:, GATES * d + g, :],
                         rhs=w_codes[:, g, :].bitcast(E4M3_X4),
                         rhs_scale=w_scales[:, g, :],
                         start=(g == 0),
@@ -189,12 +201,6 @@ def tile_graphconvolution_pb_v_kernel(
 
         def gradient(i):
             following = i + 1
-            if i >= 2:
-                multiply(i - 2)
-            if i + 2 < NODE_TILES:
-                load(i + 2)
-            if following < NODE_TILES:
-                prepare(following)
             mine = state[i]
 
             ec = []
@@ -202,35 +208,43 @@ def tile_graphconvolution_pb_v_kernel(
                 difference = three.tile([P, P, CHUNKS], F32, name="ec")
                 nc.vector.tensor_tensor(out=difference[:], in0=by_node(banks["c", d]), in1=mine["h"][:], op=ALU.subtract)
                 ec.append(difference)
+            fill_c_sum(i)
+            fill_grad_t(i)
+            fill_c_squared(i, 2)
+            if i + 2 < NODE_TILES:
+                load(i + 2)
+            if following < NODE_TILES:
+                prepare_squares(following)
+                turn_h(following)
+
             for d in range(DIRECTIONS):
                 zec = six.tile([P, P, CHUNKS], F32, name="zec")
                 nc.vector.tensor_tensor(out=zec[:], in0=by_node(banks["z", d]), in1=ec[d][:], op=ALU.mult)
                 mine["zec"].append(zec)
-            h_new = []
-            for d in range(DIRECTIONS):
-                blend = three.tile([P, P, CHUNKS], F32, name="h_new")
-                nc.vector.tensor_tensor(out=blend[:], in0=by_node(banks["c", d]), in1=mine["zec"][d][:], op=ALU.subtract)
-                h_new.append(blend)
-                if d == 0:
-                    fill_grad_t(i)
-                else:
-                    fill_c_squared(i, d)
 
-            hsum = two.tile([P, P, CHUNKS], F32, name="hsum")
-            nc.vector.tensor_tensor(out=hsum[:], in0=h_new[0][:], in1=h_new[1][:], op=ALU.add)
-            if i >= 1:
-                quantise(i - 1, 0)
-            nc.vector.tensor_tensor(out=hsum[:], in0=hsum[:], in1=h_new[2][:], op=ALU.add)
-            if i >= 1:
-                quantise(i - 1, 1)
-                quantise(i - 1, 2)
+            if i >= 2:
+                multiply(i - 2)
 
-            ds = two.tile([P, P, CHUNKS], F32, name="ds")
-            nc.vector.scalar_tensor_tensor(
-                out=ds[:], in0=hsum[:], scalar=0.0, in1=by_node(banks["grad_t"]), op0=ALU.is_gt, op1=ALU.mult
-            )
+            zec_sum = two.tile([P, P, CHUNKS], F32, name="zec_sum")
+            nc.vector.tensor_tensor(out=zec_sum[:], in0=mine["zec"][0][:], in1=mine["zec"][1][:], op=ALU.add)
+            if i >= 1:
+                quantise(i - 1, 0, 4)
+            nc.vector.tensor_tensor(out=zec_sum[:], in0=zec_sum[:], in1=mine["zec"][2][:], op=ALU.add)
+            if i >= 1:
+                quantise(i - 1, 4, 4)
+                quantise(i - 1, 8, 1)
+            if following < NODE_TILES:
+                prepare_r_factor(following)
+
+            positive = two.tile([P, P, CHUNKS], F32, name="positive")
+            nc.vector.tensor_tensor(out=positive[:], in0=by_node(banks["c_sum"]), in1=zec_sum[:], op=ALU.is_gt)
             fill_c_squared(i, 0)
+            ds = two.tile([P, P, CHUNKS], F32, name="ds")
+            nc.vector.tensor_tensor(out=ds[:], in0=by_node(banks["grad_t"]), in1=positive[:], op=ALU.mult)
+            fill_c_squared(i, 1)
 
+            dgi = two.tile([P, OPERANDS, P, CHUNKS], BF16, name="dgi", align_bytes=64)
+            mine["dgi"] = dgi
             for d in range(DIRECTIONS):
                 p = three.tile([P, P, CHUNKS], F32, name="p")
                 nc.vector.scalar_tensor_tensor(
@@ -238,12 +252,7 @@ def tile_graphconvolution_pb_v_kernel(
                 )
                 mine["p"].append(p)
                 fill_r_factor(i, d)
-                dz = three.tile([P, P, CHUNKS], BF16, name="dz", align_bytes=64)
-                nc.gpsimd.tensor_tensor(out=dz[:], in0=p[:], in1=mine["zec"][d][:], op=ALU.mult)
-                mine["dz"].append(dz)
-
-            if following < NODE_TILES:
-                turn_h(following)
+                nc.gpsimd.tensor_tensor(out=dgi[:, GATES * d + 1], in0=p[:], in1=mine["zec"][d][:], op=ALU.mult)
 
             dc_f32 = []
             for d in range(DIRECTIONS):
@@ -257,16 +266,14 @@ def tile_graphconvolution_pb_v_kernel(
                     op1=ALU.mult,
                 )
                 dc_f32.append(dc_exact)
-                dc = three.tile([P, P, CHUNKS], BF16, name="dc", align_bytes=64)
-                nc.scalar.copy(out=dc[:], in_=dc_exact[:])
-                mine["dc"].append(dc)
+                nc.scalar.copy(out=dgi[:, GATES * d + 2], in_=dc_exact[:])
                 if following < NODE_TILES:
                     fill_c(following, d)
 
             for d in range(DIRECTIONS):
-                dr = three.tile([P, P, CHUNKS], BF16, name="dr", align_bytes=64)
-                nc.vector.tensor_tensor(out=dr[:], in0=by_node(banks["r_factor", d]), in1=dc_f32[d][:], op=ALU.mult)
-                mine["dr"].append(dr)
+                nc.vector.tensor_tensor(
+                    out=dgi[:, GATES * d], in0=by_node(banks["r_factor", d]), in1=dc_f32[d][:], op=ALU.mult
+                )
                 if following < NODE_TILES:
                     fill_z(following, d)
 
@@ -278,7 +285,8 @@ def tile_graphconvolution_pb_v_kernel(
             fill_c(0, d)
         for d in range(DIRECTIONS):
             fill_z(0, d)
-        prepare(0)
+        prepare_squares(0)
+        prepare_r_factor(0)
         load(1)
         load_weights()
 
@@ -290,6 +298,7 @@ def tile_graphconvolution_pb_v_kernel(
             gradient(i)
 
         multiply(NODE_TILES - 2)
-        for d in range(DIRECTIONS):
-            quantise(NODE_TILES - 1, d)
+        quantise(NODE_TILES - 1, 0, 4)
+        quantise(NODE_TILES - 1, 4, 4)
+        quantise(NODE_TILES - 1, 8, 1)
         multiply(NODE_TILES - 1)

@@ -85,9 +85,6 @@ def tile_graphconvolution_pb_v_kernel(
 
         def prepare_squares(i):
             rows = loaded[i]
-            grad_t = two.tile([P, FEATURES], F32, name="grad_t")
-            nc.gpsimd.tensor_tensor(out=grad_t[:], in0=rows["grad"][:], in1=rows["t"][:], op=ALU.mult)
-            prepared[i]["grad_t"] = grad_t
             for d in range(DIRECTIONS):
                 c_sq = six.tile([P, FEATURES], F32, name="c_squared")
                 nc.scalar.square(c_sq[:], rows["c"][:, d, :])
@@ -100,7 +97,14 @@ def tile_graphconvolution_pb_v_kernel(
         def prepare_r_factor(i):
             for factor in prepared[i]["r_factor"]:
                 nc.scalar.activation(out=factor[:], in_=factor[:], func=FUNC.Copy, scale=-1.0, bias=0.25)
-                nc.gpsimd.tensor_tensor(out=factor[:], in0=factor[:], in1=loaded[i]["hn"][:], op=ALU.mult)
+
+        def prepare_products(i):
+            rows = loaded[i]
+            grad_t = two.tile([P, FEATURES], F32, name="grad_t")
+            nc.gpsimd.tensor_tensor(out=grad_t[:], in0=rows["grad"][:], in1=rows["t"][:], op=ALU.mult)
+            prepared[i]["grad_t"] = grad_t
+            for factor in prepared[i]["r_factor"]:
+                nc.gpsimd.tensor_tensor(out=factor[:], in0=factor[:], in1=rows["hn"][:], op=ALU.mult)
 
         def transposed(bank_name, rows):
             bank = psum.tile([P, CHUNKS, P], F32, name=bank_name)
@@ -253,6 +257,8 @@ def tile_graphconvolution_pb_v_kernel(
                 mine["p"].append(p)
                 fill_r_factor(i, d)
                 nc.gpsimd.tensor_tensor(out=dgi[:, GATES * d + 1], in0=p[:], in1=mine["zec"][d][:], op=ALU.mult)
+            if following < NODE_TILES:
+                prepare_products(following)
 
             dc_f32 = []
             for d in range(DIRECTIONS):
@@ -287,6 +293,7 @@ def tile_graphconvolution_pb_v_kernel(
             fill_z(0, d)
         prepare_squares(0)
         prepare_r_factor(0)
+        prepare_products(0)
         load(1)
         load_weights()
 

@@ -235,17 +235,20 @@ def tile_graphconvolution_pb_v_kernel(
                 quantise(i - 1, 0, 4)
             nc.vector.tensor_tensor(out=zec_sum[:], in0=zec_sum[:], in1=mine["zec"][2][:], op=ALU.add)
             if i >= 1:
-                quantise(i - 1, 4, 4)
-                quantise(i - 1, 8, 1)
+                quantise(i - 1, 4, 2)
             if following < NODE_TILES:
                 prepare_r_factor(following)
 
             positive = two.tile([P, P, CHUNKS], F32, name="positive")
             nc.vector.tensor_tensor(out=positive[:], in0=by_node(banks["c_sum"]), in1=zec_sum[:], op=ALU.is_gt)
             fill_c_squared(i, 0)
+            if i >= 1:
+                quantise(i - 1, 6, 2)
             ds = two.tile([P, P, CHUNKS], F32, name="ds")
             nc.vector.tensor_tensor(out=ds[:], in0=by_node(banks["grad_t"]), in1=positive[:], op=ALU.mult)
             fill_c_squared(i, 1)
+            if i >= 1:
+                quantise(i - 1, 8, 1)
 
             dgi = two.tile([P, OPERANDS, P, CHUNKS], BF16, name="dgi", align_bytes=64)
             mine["dgi"] = dgi

@@ -100,11 +100,14 @@ def tile_graphconvolution_pb_v_kernel(
 
         def prepare_products(i):
             rows = loaded[i]
-            grad_t = two.tile([P, FEATURES], F32, name="grad_t")
-            nc.gpsimd.tensor_tensor(out=grad_t[:], in0=rows["grad"][:], in1=rows["t"][:], op=ALU.mult)
-            prepared[i]["grad_t"] = grad_t
             for factor in prepared[i]["r_factor"]:
                 nc.gpsimd.tensor_tensor(out=factor[:], in0=factor[:], in1=rows["hn"][:], op=ALU.mult)
+
+        def prepare_grad_t(i, engine):
+            rows = loaded[i]
+            grad_t = two.tile([P, FEATURES], F32, name="grad_t")
+            engine.tensor_tensor(out=grad_t[:], in0=rows["grad"][:], in1=rows["t"][:], op=ALU.mult)
+            prepared[i]["grad_t"] = grad_t
 
         def transposed(bank_name, rows):
             bank = psum.tile([P, CHUNKS, P], F32, name=bank_name)
@@ -234,8 +237,8 @@ def tile_graphconvolution_pb_v_kernel(
             if i >= 1:
                 quantise(i - 1, 0, 4)
             nc.vector.tensor_tensor(out=zec_sum[:], in0=zec_sum[:], in1=mine["zec"][2][:], op=ALU.add)
-            if i >= 1:
-                quantise(i - 1, 4, 2)
+            if following < NODE_TILES:
+                prepare_grad_t(following, nc.vector)
             if following < NODE_TILES:
                 prepare_r_factor(following)
 
@@ -243,7 +246,7 @@ def tile_graphconvolution_pb_v_kernel(
             nc.vector.tensor_tensor(out=positive[:], in0=by_node(banks["c_sum"]), in1=zec_sum[:], op=ALU.is_gt)
             fill_c_squared(i, 0)
             if i >= 1:
-                quantise(i - 1, 6, 2)
+                quantise(i - 1, 4, 4)
             ds = two.tile([P, P, CHUNKS], F32, name="ds")
             nc.vector.tensor_tensor(out=ds[:], in0=by_node(banks["grad_t"]), in1=positive[:], op=ALU.mult)
             fill_c_squared(i, 1)
@@ -296,6 +299,7 @@ def tile_graphconvolution_pb_v_kernel(
             fill_z(0, d)
         prepare_squares(0)
         prepare_r_factor(0)
+        prepare_grad_t(0, nc.gpsimd)
         prepare_products(0)
         load(1)
         load_weights()

@@ -19,6 +19,7 @@ FEATURES = 512
 GATES = 3
 CHUNKS = FEATURES // P
 NODE_TILES = NODES // P
+FIRST_PRODUCT_STEP = 2
 OPERANDS = DIRECTIONS * GATES
 
 R_COLS = slice(0, FEATURES)
@@ -65,8 +66,8 @@ def tile_graphconvolution_pb_v_kernel(
             rows = slice(i * P, (i + 1) * P)
             tiles = {}
 
-            def fetch(name, shape, dtype, source):
-                tiles[name] = two.tile(shape, dtype, name=name + "_rows")
+            def fetch(name, shape, dtype, source, pool=two):
+                tiles[name] = pool.tile(shape, dtype, name=name + "_rows")
                 nc.sync.dma_start(out=tiles[name][:], in_=source)
 
             def gate(cols):
@@ -75,12 +76,12 @@ def tile_graphconvolution_pb_v_kernel(
             fetch("x", [P, FEATURES], BF16, x[rows, 0, :])
             fetch("c", [P, DIRECTIONS, FEATURES], F32, gate(C_COLS))
             fetch("z", [P, DIRECTIONS, FEATURES], F32, gate(Z_COLS))
-            fetch("grad", [P, FEATURES], BF16, grad_out[rows, 0, :])
-            fetch("t", [P, FEATURES], F32, t[rows, 0, :])
+            fetch("grad", [P, FEATURES], BF16, grad_out[rows, 0, :], pool=three)
+            fetch("t", [P, FEATURES], F32, t[rows, 0, :], pool=three)
             fetch("r", [P, DIRECTIONS, FEATURES], F32, gate(R_COLS))
             fetch("hn", [P, FEATURES], F32, hn[0, rows, :])
             loaded[i] = tiles
-            prepared[i] = {"c_squared": [], "r_factor": []}
+            prepared[i] = {"c_squared": []}
             state[i] = {"zec": [], "p": []}
 
         def prepare_squares(i):
@@ -89,24 +90,25 @@ def tile_graphconvolution_pb_v_kernel(
                 c_sq = six.tile([P, FEATURES], F32, name="c_squared")
                 nc.scalar.square(c_sq[:], rows["c"][:, d, :])
                 prepared[i]["c_squared"].append(c_sq)
+            factor = two.tile([P, DIRECTIONS, FEATURES], F32, name="r_factor")
             for d in range(DIRECTIONS):
-                factor = six.tile([P, FEATURES], F32, name="r_factor")
-                nc.scalar.activation(out=factor[:], in_=rows["r"][:, d, :], func=FUNC.Square, bias=-0.5, scale=1.0)
-                prepared[i]["r_factor"].append(factor)
+                nc.scalar.activation(out=factor[:, d, :], in_=rows["r"][:, d, :], func=FUNC.Square, bias=-0.5, scale=1.0)
+            prepared[i]["r_factor"] = factor
 
         def prepare_r_factor(i):
-            for factor in prepared[i]["r_factor"]:
-                nc.scalar.activation(out=factor[:], in_=factor[:], func=FUNC.Copy, scale=-1.0, bias=0.25)
+            factor = prepared[i]["r_factor"]
+            for d in range(DIRECTIONS):
+                nc.scalar.activation(out=factor[:, d, :], in_=factor[:, d, :], func=FUNC.Copy, scale=-1.0, bias=0.25)
 
         def prepare_products(i):
-            rows = loaded[i]
-            for factor in prepared[i]["r_factor"]:
-                nc.gpsimd.tensor_tensor(out=factor[:], in0=factor[:], in1=rows["hn"][:], op=ALU.mult)
+            factor = prepared[i]["r_factor"]
+            hn_for_all = loaded[i]["hn"][:].unsqueeze(1).to_broadcast([P, DIRECTIONS, FEATURES])
+            nc.gpsimd.tensor_tensor(out=factor[:], in0=factor[:], in1=hn_for_all, op=ALU.mult)
 
-        def prepare_grad_t(i, engine):
+        def prepare_grad_t(i):
             rows = loaded[i]
             grad_t = two.tile([P, FEATURES], F32, name="grad_t")
-            engine.tensor_tensor(out=grad_t[:], in0=rows["grad"][:], in1=rows["t"][:], op=ALU.mult)
+            nc.vector.tensor_tensor(out=grad_t[:], in0=rows["grad"][:], in1=rows["t"][:], op=ALU.mult)
             prepared[i]["grad_t"] = grad_t
 
         def transposed(bank_name, rows):
@@ -143,7 +145,7 @@ def tile_graphconvolution_pb_v_kernel(
             banks["z", d] = transposed("b%d" % d, loaded[i]["z"][:, d, :])
 
         def fill_r_factor(i, d):
-            banks["r_factor", d] = transposed("b%d" % d, prepared[i]["r_factor"][d][:])
+            banks["r_factor", d] = transposed("b%d" % d, prepared[i]["r_factor"][:, d, :])
 
         def turn_h(i):
             bank = psum_pair.tile([P, CHUNKS, P], BF16, name="pair")
@@ -216,7 +218,6 @@ def tile_graphconvolution_pb_v_kernel(
                 nc.vector.tensor_tensor(out=difference[:], in0=by_node(banks["c", d]), in1=mine["h"][:], op=ALU.subtract)
                 ec.append(difference)
             fill_c_sum(i)
-            fill_grad_t(i)
             fill_c_squared(i, 2)
             if i + 2 < NODE_TILES:
                 load(i + 2)
@@ -229,16 +230,18 @@ def tile_graphconvolution_pb_v_kernel(
                 nc.vector.tensor_tensor(out=zec[:], in0=by_node(banks["z", d]), in1=ec[d][:], op=ALU.mult)
                 mine["zec"].append(zec)
 
-            if i >= 2:
-                multiply(i - 2)
+            if i == FIRST_PRODUCT_STEP:
+                quantise_weights()
+            if i >= FIRST_PRODUCT_STEP:
+                multiply(i - FIRST_PRODUCT_STEP)
 
             zec_sum = two.tile([P, P, CHUNKS], F32, name="zec_sum")
             nc.vector.tensor_tensor(out=zec_sum[:], in0=mine["zec"][0][:], in1=mine["zec"][1][:], op=ALU.add)
+            prepare_grad_t(i)
+            fill_grad_t(i)
+            nc.vector.tensor_tensor(out=zec_sum[:], in0=zec_sum[:], in1=mine["zec"][2][:], op=ALU.add)
             if i >= 1:
                 quantise(i - 1, 0, 4)
-            nc.vector.tensor_tensor(out=zec_sum[:], in0=zec_sum[:], in1=mine["zec"][2][:], op=ALU.add)
-            if following < NODE_TILES:
-                prepare_grad_t(following, nc.vector)
             if following < NODE_TILES:
                 prepare_r_factor(following)
 
@@ -299,16 +302,13 @@ def tile_graphconvolution_pb_v_kernel(
             fill_z(0, d)
         prepare_squares(0)
         prepare_r_factor(0)
-        prepare_grad_t(0, nc.gpsimd)
         prepare_products(0)
         load(1)
         load_weights()
 
         gradient(0)
         regroup_weights()
-        gradient(1)
-        quantise_weights()
-        for i in range(2, NODE_TILES):
+        for i in range(1, NODE_TILES):
             gradient(i)
 
         multiply(NODE_TILES - 2)

@@ -21,6 +21,9 @@ CHUNKS = FEATURES // P
 NODE_TILES = NODES // P
 FIRST_PRODUCT_STEP = 2
 OPERANDS = DIRECTIONS * GATES
+GATE_AT = (1, 2, 0)
+DZ_AT, DC_AT, DR_AT = 0, DIRECTIONS, 2 * DIRECTIONS
+QUANTISE_CALLS = ((0, 4), (4, 2), (6, 2), (8, 1))
 
 R_COLS = slice(0, FEATURES)
 Z_COLS = slice(FEATURES, 2 * FEATURES)
@@ -44,6 +47,7 @@ def tile_graphconvolution_pb_v_kernel(
     tc, agg, x, wih, whh, bih, bhh, wh, bh, gates, hn, t, grad_out, out
 ):
     nc = tc.nc
+    ALL = slice(0, DIRECTIONS)
     with ExitStack() as ctx:
         once = ctx.enter_context(tc.tile_pool(name="once", bufs=1))
         two = ctx.enter_context(tc.tile_pool(name="two", bufs=2))
@@ -57,6 +61,7 @@ def tile_graphconvolution_pb_v_kernel(
         identity_bf16 = once.tile([P, P], BF16, name="identity_bf16")
         make_identity(nc, identity_bf16[:])
 
+        x_rows = {}
         loaded = {}
         prepared = {}
         banks = {}
@@ -66,20 +71,34 @@ def tile_graphconvolution_pb_v_kernel(
             rows = slice(i * P, (i + 1) * P)
             tiles = {}
 
-            def fetch(name, shape, dtype, source, pool=two):
-                tiles[name] = pool.tile(shape, dtype, name=name + "_rows")
-                nc.sync.dma_start(out=tiles[name][:], in_=source)
+            def fetch(pool, name, dtype, source):
+                tile = pool.tile([P, FEATURES], dtype, name=name + "_rows")
+                nc.sync.dma_start(out=tile[:], in_=source)
+                return tile
 
-            def gate(cols):
-                return gates[:, 0, rows, cols].rearrange("d n k -> n d k")
+            def gate(name, cols):
+                return [fetch(six, name, F32, gates[d, 0, rows, cols]) for d in range(DIRECTIONS)]
 
-            fetch("x", [P, FEATURES], BF16, x[rows, 0, :])
-            fetch("c", [P, DIRECTIONS, FEATURES], F32, gate(C_COLS))
-            fetch("z", [P, DIRECTIONS, FEATURES], F32, gate(Z_COLS))
-            fetch("grad", [P, FEATURES], BF16, grad_out[rows, 0, :], pool=three)
-            fetch("t", [P, FEATURES], F32, t[rows, 0, :], pool=three)
-            fetch("r", [P, DIRECTIONS, FEATURES], F32, gate(R_COLS))
-            fetch("hn", [P, FEATURES], F32, hn[0, rows, :])
+            def product_inputs():
+                tiles["grad"] = fetch(two, "grad", BF16, grad_out[rows, 0, :])
+                tiles["t"] = fetch(two, "t", F32, t[rows, 0, :])
+
+            def load_x(j):
+                x_rows[j] = fetch(two, "x", BF16, x[j * P : (j + 1) * P, 0, :])
+
+            if i > 0:
+                product_inputs()
+            if i not in x_rows:
+                load_x(i)
+            tiles["x"] = x_rows[i]
+            tiles["c"] = gate("c", C_COLS)
+            if i == 0:
+                load_x(1)
+            tiles["z"] = gate("z", Z_COLS)
+            if i == 0:
+                product_inputs()
+            tiles["hn"] = fetch(two, "hn", F32, hn[0, rows, :])
+            tiles["r"] = gate("r", R_COLS)
             loaded[i] = tiles
             prepared[i] = {"c_squared": []}
             state[i] = {"zec": [], "p": []}
@@ -88,27 +107,33 @@ def tile_graphconvolution_pb_v_kernel(
             rows = loaded[i]
             for d in range(DIRECTIONS):
                 c_sq = six.tile([P, FEATURES], F32, name="c_squared")
-                nc.scalar.square(c_sq[:], rows["c"][:, d, :])
+                nc.scalar.square(c_sq[:], rows["c"][d][:])
                 prepared[i]["c_squared"].append(c_sq)
-            factor = two.tile([P, DIRECTIONS, FEATURES], F32, name="r_factor")
-            for d in range(DIRECTIONS):
-                nc.scalar.activation(out=factor[:, d, :], in_=rows["r"][:, d, :], func=FUNC.Square, bias=-0.5, scale=1.0)
-            prepared[i]["r_factor"] = factor
+            prepared[i]["r_factor"] = two.tile([P, DIRECTIONS, FEATURES], F32, name="r_factor")
+            for d in some_directions(ALL):
+                square_r(i, d)
 
-        def prepare_r_factor(i):
+        def some_directions(which):
+            return range(which.start, which.stop)
+
+        def square_r(i, d):
             factor = prepared[i]["r_factor"]
-            for d in range(DIRECTIONS):
+            nc.scalar.activation(out=factor[:, d, :], in_=loaded[i]["r"][d][:], func=FUNC.Square, bias=-0.5, scale=1.0)
+
+        def prepare_r_factor(i, which):
+            factor = prepared[i]["r_factor"]
+            for d in some_directions(which):
                 nc.scalar.activation(out=factor[:, d, :], in_=factor[:, d, :], func=FUNC.Copy, scale=-1.0, bias=0.25)
 
-        def prepare_products(i):
-            factor = prepared[i]["r_factor"]
-            hn_for_all = loaded[i]["hn"][:].unsqueeze(1).to_broadcast([P, DIRECTIONS, FEATURES])
-            nc.gpsimd.tensor_tensor(out=factor[:], in0=factor[:], in1=hn_for_all, op=ALU.mult)
+        def prepare_products(i, which):
+            factor = prepared[i]["r_factor"][:, which, :]
+            hn_for_each = loaded[i]["hn"][:].unsqueeze(1).to_broadcast([P, which.stop - which.start, FEATURES])
+            nc.gpsimd.tensor_tensor(out=factor, in0=factor, in1=hn_for_each, op=ALU.mult)
 
-        def prepare_grad_t(i):
+        def prepare_grad_t(i, engine):
             rows = loaded[i]
-            grad_t = two.tile([P, FEATURES], F32, name="grad_t")
-            nc.vector.tensor_tensor(out=grad_t[:], in0=rows["grad"][:], in1=rows["t"][:], op=ALU.mult)
+            grad_t = once.tile([P, FEATURES], F32, name="positive_or_grad_t")
+            engine.tensor_tensor(out=grad_t[:], in0=rows["grad"][:], in1=rows["t"][:], op=ALU.mult)
             prepared[i]["grad_t"] = grad_t
 
         def transposed(bank_name, rows):
@@ -119,7 +144,7 @@ def tile_graphconvolution_pb_v_kernel(
             return bank
 
         def fill_c(i, d):
-            banks["c", d] = transposed("a%d" % d, loaded[i]["c"][:, d, :])
+            banks["c", d] = transposed("a%d" % d, loaded[i]["c"][d][:])
 
         def fill_c_sum(i):
             bank = psum.tile([P, CHUNKS, P], F32, name="a0")
@@ -127,7 +152,7 @@ def tile_graphconvolution_pb_v_kernel(
                 for d in range(DIRECTIONS):
                     nc.tensor.matmul(
                         bank[:, chunk, :],
-                        lhsT=loaded[i]["c"][:, d, chunk * P : (chunk + 1) * P],
+                        lhsT=loaded[i]["c"][d][:, chunk * P : (chunk + 1) * P],
                         rhs=identity[:],
                         is_transpose=True,
                         start=(d == 0),
@@ -142,7 +167,7 @@ def tile_graphconvolution_pb_v_kernel(
             banks["c_squared", d] = transposed("a%d" % d, prepared[i]["c_squared"][d][:])
 
         def fill_z(i, d):
-            banks["z", d] = transposed("b%d" % d, loaded[i]["z"][:, d, :])
+            banks["z", d] = transposed("b%d" % d, loaded[i]["z"][d][:])
 
         def fill_r_factor(i, d):
             banks["r_factor", d] = transposed("b%d" % d, prepared[i]["r_factor"][:, d, :])
@@ -179,7 +204,8 @@ def tile_graphconvolution_pb_v_kernel(
                     in_=w_grouped[:, g].rearrange("p n t -> p (n t)"),
                 )
 
-        def quantise(i, first, count):
+        def quantise(i, call):
+            first, count = QUANTISE_CALLS[call]
             if first == 0:
                 state[i]["codes"] = two.tile([P, OPERANDS, P], U32, name="codes", align_bytes=64)
                 state[i]["scales"] = two.tile([P, OPERANDS, P], U8, name="scales", align_bytes=64)
@@ -190,40 +216,61 @@ def tile_graphconvolution_pb_v_kernel(
                 in_=state[i]["dgi"][:, some].rearrange("p u n t -> p (u n t)"),
             )
 
+        def product_pass(i, d, place, acc):
+            g = GATE_AT[place]
+            nc.tensor.matmul_mx(
+                out=acc[:],
+                lhsT=state[i]["codes"][:, DIRECTIONS * place + d, :].bitcast(E5M2_X4),
+                lhsT_scale=state[i]["scales"][:, DIRECTIONS * place + d, :],
+                rhs=w_codes[:, g, :].bitcast(E4M3_X4),
+                rhs_scale=w_scales[:, g, :],
+                start=(place == 0),
+                stop=(place == GATES - 1),
+            )
+
+        def store(i, d, acc, by_vector=False):
+            result = six.tile([P, FEATURES], F32, name="result")
+            if by_vector:
+                nc.vector.tensor_copy(out=result[:], in_=acc[:])
+            else:
+                nc.scalar.copy(out=result[:], in_=acc[:])
+            nc.scalar.dma_start(out=out[d, 0, i * P : (i + 1) * P, :], in_=result[:])
+
         def multiply(i):
-            rows = slice(i * P, (i + 1) * P)
             for d in range(DIRECTIONS):
                 acc = psum_pair.tile([P, FEATURES], F32, name="pair")
-                for g in range(GATES):
-                    nc.tensor.matmul_mx(
-                        out=acc[:],
-                        lhsT=state[i]["codes"][:, GATES * d + g, :].bitcast(E5M2_X4),
-                        lhsT_scale=state[i]["scales"][:, GATES * d + g, :],
-                        rhs=w_codes[:, g, :].bitcast(E4M3_X4),
-                        rhs_scale=w_scales[:, g, :],
-                        start=(g == 0),
-                        stop=(g == GATES - 1),
-                    )
-                result = three.tile([P, FEATURES], F32, name="result")
-                nc.scalar.copy(out=result[:], in_=acc[:])
-                nc.scalar.dma_start(out=out[d, 0, rows, :], in_=result[:])
+                for place in range(GATES):
+                    product_pass(i, d, place, acc)
+                store(i, d, acc)
+
+        def quantise_and_multiply(i, call, accs):
+            quantise(i, call)
+            first, count = QUANTISE_CALLS[call]
+            for operand in range(first, first + count):
+                place, d = divmod(operand, DIRECTIONS)
+                product_pass(i, d, place, accs[d])
+                if place == GATES - 1:
+                    store(i, d, accs[d], by_vector=(d == DIRECTIONS - 1))
 
         def gradient(i):
             following = i + 1
+            is_last = following == NODE_TILES
             mine = state[i]
 
+            if not is_last:
+                turn_h(following)
             ec = []
             for d in range(DIRECTIONS):
                 difference = three.tile([P, P, CHUNKS], F32, name="ec")
                 nc.vector.tensor_tensor(out=difference[:], in0=by_node(banks["c", d]), in1=mine["h"][:], op=ALU.subtract)
                 ec.append(difference)
             fill_c_sum(i)
+            fill_grad_t(i)
             fill_c_squared(i, 2)
             if i + 2 < NODE_TILES:
                 load(i + 2)
-            if following < NODE_TILES:
+            if not is_last:
                 prepare_squares(following)
-                turn_h(following)
 
             for d in range(DIRECTIONS):
                 zec = six.tile([P, P, CHUNKS], F32, name="zec")
@@ -237,24 +284,26 @@ def tile_graphconvolution_pb_v_kernel(
 
             zec_sum = two.tile([P, P, CHUNKS], F32, name="zec_sum")
             nc.vector.tensor_tensor(out=zec_sum[:], in0=mine["zec"][0][:], in1=mine["zec"][1][:], op=ALU.add)
-            prepare_grad_t(i)
-            fill_grad_t(i)
+            if i >= 1:
+                quantise(i - 1, 0)
             nc.vector.tensor_tensor(out=zec_sum[:], in0=zec_sum[:], in1=mine["zec"][2][:], op=ALU.add)
             if i >= 1:
-                quantise(i - 1, 0, 4)
-            if following < NODE_TILES:
-                prepare_r_factor(following)
+                quantise(i - 1, 1)
+            if not is_last:
+                prepare_r_factor(following, ALL)
 
-            positive = two.tile([P, P, CHUNKS], F32, name="positive")
+            positive = once.tile([P, P, CHUNKS], F32, name="positive_or_grad_t")
             nc.vector.tensor_tensor(out=positive[:], in0=by_node(banks["c_sum"]), in1=zec_sum[:], op=ALU.is_gt)
             fill_c_squared(i, 0)
             if i >= 1:
-                quantise(i - 1, 4, 4)
+                quantise(i - 1, 2)
             ds = two.tile([P, P, CHUNKS], F32, name="ds")
             nc.vector.tensor_tensor(out=ds[:], in0=by_node(banks["grad_t"]), in1=positive[:], op=ALU.mult)
             fill_c_squared(i, 1)
             if i >= 1:
-                quantise(i - 1, 8, 1)
+                quantise(i - 1, 3)
+            if not is_last:
+                prepare_grad_t(following, nc.gpsimd)
 
             dgi = two.tile([P, OPERANDS, P, CHUNKS], BF16, name="dgi", align_bytes=64)
             mine["dgi"] = dgi
@@ -265,9 +314,9 @@ def tile_graphconvolution_pb_v_kernel(
                 )
                 mine["p"].append(p)
                 fill_r_factor(i, d)
-                nc.gpsimd.tensor_tensor(out=dgi[:, GATES * d + 1], in0=p[:], in1=mine["zec"][d][:], op=ALU.mult)
-            if following < NODE_TILES:
-                prepare_products(following)
+                nc.gpsimd.tensor_tensor(out=dgi[:, DZ_AT + d], in0=p[:], in1=mine["zec"][d][:], op=ALU.mult)
+            if not is_last:
+                prepare_products(following, ALL)
 
             dc_f32 = []
             for d in range(DIRECTIONS):
@@ -281,16 +330,24 @@ def tile_graphconvolution_pb_v_kernel(
                     op1=ALU.mult,
                 )
                 dc_f32.append(dc_exact)
-                nc.scalar.copy(out=dgi[:, GATES * d + 2], in_=dc_exact[:])
-                if following < NODE_TILES:
+                nc.scalar.copy(out=dgi[:, DC_AT + d], in_=dc_exact[:])
+                if not is_last:
                     fill_c(following, d)
 
+            if is_last:
+                multiply(i - 1)
+                accs = [psum.tile([P, FEATURES], F32, name="a%d" % d) for d in range(DIRECTIONS)]
             for d in range(DIRECTIONS):
                 nc.vector.tensor_tensor(
-                    out=dgi[:, GATES * d], in0=by_node(banks["r_factor", d]), in1=dc_f32[d][:], op=ALU.mult
+                    out=dgi[:, DR_AT + d], in0=by_node(banks["r_factor", d]), in1=dc_f32[d][:], op=ALU.mult
                 )
-                if following < NODE_TILES:
+                if not is_last:
                     fill_z(following, d)
+                elif d >= 1:
+                    quantise_and_multiply(i, d - 1, accs)
+            if is_last:
+                quantise_and_multiply(i, 2, accs)
+                quantise_and_multiply(i, 3, accs)
 
         ctx.enter_context(tc.manual_schedule())
 
@@ -300,9 +357,11 @@ def tile_graphconvolution_pb_v_kernel(
             fill_c(0, d)
         for d in range(DIRECTIONS):
             fill_z(0, d)
+        prepare_grad_t(0, nc.gpsimd)
         prepare_squares(0)
-        prepare_r_factor(0)
-        prepare_products(0)
+        for d in range(DIRECTIONS):
+            prepare_r_factor(0, slice(d, d + 1))
+            prepare_products(0, slice(d, d + 1))
         load(1)
         load_weights()
 
@@ -310,9 +369,3 @@ def tile_graphconvolution_pb_v_kernel(
         regroup_weights()
         for i in range(1, NODE_TILES):
             gradient(i)
-
-        multiply(NODE_TILES - 2)
-        quantise(NODE_TILES - 1, 0, 4)
-        quantise(NODE_TILES - 1, 4, 4)
-        quantise(NODE_TILES - 1, 8, 1)
-        multiply(NODE_TILES - 1)

@@ -19,7 +19,7 @@ FEATURES = 512
 GATES = 3
 CHUNKS = FEATURES // P
 NODE_TILES = NODES // P
-FIRST_PRODUCT_STEP = 2
+FIRST_PRODUCT_STEP = 3
 OPERANDS = DIRECTIONS * GATES
 GATE_AT = (1, 2, 0)
 DZ_AT, DC_AT, DR_AT = 0, DIRECTIONS, 2 * DIRECTIONS
@@ -48,6 +48,7 @@ def tile_graphconvolution_pb_v_kernel(
 ):
     nc = tc.nc
     ALL = slice(0, DIRECTIONS)
+    REGROUP = {(1, "C"): (0,), (2, "A"): (1,), (2, "B"): (2,)}
     with ExitStack() as ctx:
         once = ctx.enter_context(tc.tile_pool(name="once", bufs=1))
         two = ctx.enter_context(tc.tile_pool(name="two", bufs=2))
@@ -61,6 +62,7 @@ def tile_graphconvolution_pb_v_kernel(
         identity_bf16 = once.tile([P, P], BF16, name="identity_bf16")
         make_identity(nc, identity_bf16[:])
 
+        waiting = []
         x_rows = {}
         loaded = {}
         prepared = {}
@@ -110,8 +112,6 @@ def tile_graphconvolution_pb_v_kernel(
                 nc.scalar.square(c_sq[:], rows["c"][d][:])
                 prepared[i]["c_squared"].append(c_sq)
             prepared[i]["r_factor"] = two.tile([P, DIRECTIONS, FEATURES], F32, name="r_factor")
-            for d in some_directions(ALL):
-                square_r(i, d)
 
         def some_directions(which):
             return range(which.start, which.stop)
@@ -192,9 +192,8 @@ def tile_graphconvolution_pb_v_kernel(
                 out=w_rows[:], in_=wih.rearrange("(g t p) n -> p g t n", t=CHUNKS, p=P)
             )
 
-        def regroup_weights():
-            for g in range(GATES):
-                nc.scalar.copy(out=w_grouped[:, g], in_=w_rows[:, g].rearrange("p t n -> p n t"))
+        def regroup_weights(g):
+            nc.scalar.copy(out=w_grouped[:, g], in_=w_rows[:, g].rearrange("p t n -> p n t"))
 
         def quantise_weights():
             for g in range(GATES):
@@ -207,8 +206,8 @@ def tile_graphconvolution_pb_v_kernel(
         def quantise(i, call):
             first, count = QUANTISE_CALLS[call]
             if first == 0:
-                state[i]["codes"] = two.tile([P, OPERANDS, P], U32, name="codes", align_bytes=64)
-                state[i]["scales"] = two.tile([P, OPERANDS, P], U8, name="scales", align_bytes=64)
+                state[i]["codes"] = three.tile([P, OPERANDS, P], U32, name="codes", align_bytes=64)
+                state[i]["scales"] = three.tile([P, OPERANDS, P], U8, name="scales", align_bytes=64)
             some = slice(first, first + count)
             nc.vector.quantize_mx(
                 out=state[i]["codes"][:, some, :].rearrange("p u n -> p (u n)").bitcast(E5M2_X4),
@@ -236,12 +235,11 @@ def tile_graphconvolution_pb_v_kernel(
                 nc.scalar.copy(out=result[:], in_=acc[:])
             nc.scalar.dma_start(out=out[d, 0, i * P : (i + 1) * P, :], in_=result[:])
 
-        def multiply(i):
-            for d in range(DIRECTIONS):
-                acc = psum_pair.tile([P, FEATURES], F32, name="pair")
-                for place in range(GATES):
-                    product_pass(i, d, place, acc)
-                store(i, d, acc)
+        def multiply(i, d):
+            acc = psum_pair.tile([P, FEATURES], F32, name="pair")
+            for place in range(GATES):
+                product_pass(i, d, place, acc)
+            store(i, d, acc)
 
         def quantise_and_multiply(i, call, accs):
             quantise(i, call)
@@ -269,9 +267,13 @@ def tile_graphconvolution_pb_v_kernel(
             fill_c_squared(i, 2)
             if i + 2 < NODE_TILES:
                 load(i + 2)
+            if i == 0:
+                load_weights()
             if not is_last:
                 prepare_squares(following)
 
+            for g in REGROUP.get((i, "A"), ()):
+                regroup_weights(g)
             for d in range(DIRECTIONS):
                 zec = six.tile([P, P, CHUNKS], F32, name="zec")
                 nc.vector.tensor_tensor(out=zec[:], in0=by_node(banks["z", d]), in1=ec[d][:], op=ALU.mult)
@@ -279,8 +281,15 @@ def tile_graphconvolution_pb_v_kernel(
 
             if i == FIRST_PRODUCT_STEP:
                 quantise_weights()
-            if i >= FIRST_PRODUCT_STEP:
-                multiply(i - FIRST_PRODUCT_STEP)
+            if i >= 2:
+                waiting.extend((i - 2, d) for d in range(DIRECTIONS))
+            turns = min(len(waiting), 4) if i >= FIRST_PRODUCT_STEP else 0
+            for turn in range(max(turns, DIRECTIONS)):
+                if turn < turns:
+                    multiply(*waiting[turn])
+                if not is_last and turn < DIRECTIONS:
+                    square_r(following, turn)
+            waiting[:] = waiting[turns:]
 
             zec_sum = two.tile([P, P, CHUNKS], F32, name="zec_sum")
             nc.vector.tensor_tensor(out=zec_sum[:], in0=mine["zec"][0][:], in1=mine["zec"][1][:], op=ALU.add)
@@ -291,6 +300,8 @@ def tile_graphconvolution_pb_v_kernel(
                 quantise(i - 1, 1)
             if not is_last:
                 prepare_r_factor(following, ALL)
+            for g in REGROUP.get((i, "B"), ()):
+                regroup_weights(g)
 
             positive = once.tile([P, P, CHUNKS], F32, name="positive_or_grad_t")
             nc.vector.tensor_tensor(out=positive[:], in0=by_node(banks["c_sum"]), in1=zec_sum[:], op=ALU.is_gt)
@@ -334,8 +345,11 @@ def tile_graphconvolution_pb_v_kernel(
                 if not is_last:
                     fill_c(following, d)
 
+            for g in REGROUP.get((i, "C"), ()):
+                regroup_weights(g)
             if is_last:
-                multiply(i - 1)
+                for d in range(DIRECTIONS):
+                    multiply(i - 1, d)
                 accs = [psum.tile([P, FEATURES], F32, name="a%d" % d) for d in range(DIRECTIONS)]
             for d in range(DIRECTIONS):
                 nc.vector.tensor_tensor(
@@ -360,12 +374,11 @@ def tile_graphconvolution_pb_v_kernel(
         prepare_grad_t(0, nc.gpsimd)
         prepare_squares(0)
         for d in range(DIRECTIONS):
+            square_r(0, d)
             prepare_r_factor(0, slice(d, d + 1))
             prepare_products(0, slice(d, d + 1))
         load(1)
-        load_weights()
 
         gradient(0)
-        regroup_weights()
         for i in range(1, NODE_TILES):
             gradient(i)

@@ -96,11 +96,13 @@ def tile_graphconvolution_pb_v_kernel(
             tiles["c"] = gate("c", C_COLS)
             if i == 0:
                 load_x(1)
-            tiles["z"] = gate("z", Z_COLS)
             if i == 0:
+                tiles["z"] = gate("z", Z_COLS)
                 product_inputs()
             tiles["hn"] = fetch(two, "hn", F32, hn[0, rows, :])
             tiles["r"] = gate("r", R_COLS)
+            if i > 0:
+                tiles["z"] = gate("z", Z_COLS)
             loaded[i] = tiles
             prepared[i] = {"c_squared": []}
             state[i] = {"zec": [], "p": []}

@@ -235,7 +235,7 @@ def tile_graphconvolution_pb_v_kernel(
                 nc.vector.tensor_copy(out=result[:], in_=acc[:])
             else:
                 nc.scalar.copy(out=result[:], in_=acc[:])
-            nc.scalar.dma_start(out=out[d, 0, i * P : (i + 1) * P, :], in_=result[:])
+            nc.sync.dma_start(out=out[d, 0, i * P : (i + 1) * P, :], in_=result[:])
 
         def multiply(i, d):
             acc = psum_pair.tile([P, FEATURES], F32, name="pair")

@@ -19,6 +19,7 @@ FEATURES = 512
 GATES = 3
 CHUNKS = FEATURES // P
 NODE_TILES = NODES // P
+SEPARATE_LOADS = 2
 FIRST_PRODUCT_STEP = 3
 OPERANDS = DIRECTIONS * GATES
 GATE_AT = (1, 2, 0)
@@ -79,7 +80,13 @@ def tile_graphconvolution_pb_v_kernel(
                 return tile
 
             def gate(name, cols):
-                return [fetch(six, name, F32, gates[d, 0, rows, cols]) for d in range(DIRECTIONS)]
+                tile = two.tile([P, DIRECTIONS, FEATURES], F32, name=name + "_rows")
+                if i < SEPARATE_LOADS:
+                    for d in range(DIRECTIONS):
+                        nc.sync.dma_start(out=tile[:, d, :], in_=gates[d, 0, rows, cols])
+                else:
+                    nc.sync.dma_start(out=tile[:], in_=gates[:, 0, rows, cols].rearrange("d n f -> n d f"))
+                return [tile[:, d, :] for d in range(DIRECTIONS)]
 
             def product_inputs():
                 tiles["grad"] = fetch(two, "grad", BF16, grad_out[rows, 0, :])
@@ -132,6 +139,12 @@ def tile_graphconvolution_pb_v_kernel(
             hn_for_each = loaded[i]["hn"][:].unsqueeze(1).to_broadcast([P, which.stop - which.start, FEATURES])
             nc.gpsimd.tensor_tensor(out=factor, in0=factor, in1=hn_for_each, op=ALU.mult)
 
+        def r_product_by_vector(i, d):
+            factor = prepared[i]["r_factor"][:, d, :]
+            nc.vector.scalar_tensor_tensor(
+                out=factor, in0=factor, scalar=0.25, in1=loaded[i]["hn"][:], op0=ALU.subtract, op1=ALU.mult
+            )
+
         def prepare_grad_t(i, engine):
             rows = loaded[i]
             grad_t = once.tile([P, FEATURES], F32, name="positive_or_grad_t")
@@ -180,8 +193,11 @@ def tile_graphconvolution_pb_v_kernel(
                 nc.tensor.transpose(
                     bank[:, chunk, :], loaded[i]["x"][:, chunk * P : (chunk + 1) * P], identity_bf16[:]
                 )
+            banks["h"] = bank
+
+        def fetch_h(i):
             h = two.tile([P, P, CHUNKS], BF16, name="h")
-            nc.scalar.copy(out=h[:], in_=by_node(bank))
+            nc.scalar.copy(out=h[:], in_=by_node(banks["h"]))
             state[i]["h"] = h
 
         w_rows = once.tile([P, GATES, CHUNKS, FEATURES], BF16, name="w_rows")
@@ -265,14 +281,14 @@ def tile_graphconvolution_pb_v_kernel(
                 nc.vector.tensor_tensor(out=difference[:], in0=by_node(banks["c", d]), in1=mine["h"][:], op=ALU.subtract)
                 ec.append(difference)
             fill_c_sum(i)
-            fill_grad_t(i)
+            if i > 0:
+                fill_grad_t(i)
             fill_c_squared(i, 2)
-            if i + 2 < NODE_TILES:
+            if 0 < i < NODE_TILES - 2:
                 load(i + 2)
-            if i == 0:
-                load_weights()
             if not is_last:
                 prepare_squares(following)
+                fetch_h(following)
 
             for g in REGROUP.get((i, "A"), ()):
                 regroup_weights(g)
@@ -293,11 +309,16 @@ def tile_graphconvolution_pb_v_kernel(
                     square_r(following, turn)
             waiting[:] = waiting[turns:]
 
+            if i == 0:
+                prepare_grad_t(0, nc.vector)
+                fill_grad_t(0)
             zec_sum = two.tile([P, P, CHUNKS], F32, name="zec_sum")
             nc.vector.tensor_tensor(out=zec_sum[:], in0=mine["zec"][0][:], in1=mine["zec"][1][:], op=ALU.add)
             if i >= 1:
                 quantise(i - 1, 0)
             nc.vector.tensor_tensor(out=zec_sum[:], in0=zec_sum[:], in1=mine["zec"][2][:], op=ALU.add)
+            if i == 0:
+                r_product_by_vector(0, 0)
             if i >= 1:
                 quantise(i - 1, 1)
             if not is_last:
@@ -308,11 +329,17 @@ def tile_graphconvolution_pb_v_kernel(
             positive = once.tile([P, P, CHUNKS], F32, name="positive_or_grad_t")
             nc.vector.tensor_tensor(out=positive[:], in0=by_node(banks["c_sum"]), in1=zec_sum[:], op=ALU.is_gt)
             fill_c_squared(i, 0)
+            if i == 0:
+                r_product_by_vector(0, 1)
             if i >= 1:
                 quantise(i - 1, 2)
             ds = two.tile([P, P, CHUNKS], F32, name="ds")
             nc.vector.tensor_tensor(out=ds[:], in0=by_node(banks["grad_t"]), in1=positive[:], op=ALU.mult)
             fill_c_squared(i, 1)
+            if i == 0:
+                r_product_by_vector(0, 2)
+                load(2)
+                load_weights()
             if i >= 1:
                 quantise(i - 1, 3)
             if not is_last:
@@ -354,9 +381,14 @@ def tile_graphconvolution_pb_v_kernel(
                     multiply(i - 1, d)
                 accs = [psum.tile([P, FEATURES], F32, name="a%d" % d) for d in range(DIRECTIONS)]
             for d in range(DIRECTIONS):
-                nc.vector.tensor_tensor(
-                    out=dgi[:, DR_AT + d], in0=by_node(banks["r_factor", d]), in1=dc_f32[d][:], op=ALU.mult
-                )
+                if i == 0:
+                    nc.vector.scalar_tensor_tensor(
+                        out=dgi[:, DR_AT + d], in0=by_node(banks["r_factor", d]), scalar=-1.0, in1=dc_f32[d][:], op0=ALU.mult, op1=ALU.mult
+                    )
+                else:
+                    nc.vector.tensor_tensor(
+                        out=dgi[:, DR_AT + d], in0=by_node(banks["r_factor", d]), in1=dc_f32[d][:], op=ALU.mult
+                    )
                 if not is_last:
                     fill_z(following, d)
                 elif d >= 1:
@@ -369,16 +401,14 @@ def tile_graphconvolution_pb_v_kernel(
 
         load(0)
         turn_h(0)
+        fetch_h(0)
         for d in range(DIRECTIONS):
             fill_c(0, d)
         for d in range(DIRECTIONS):
             fill_z(0, d)
-        prepare_grad_t(0, nc.gpsimd)
         prepare_squares(0)
         for d in range(DIRECTIONS):
             square_r(0, d)
-            prepare_r_factor(0, slice(d, d + 1))
-            prepare_products(0, slice(d, d + 1))
         load(1)
 
         gradient(0)

@@ -19,6 +19,7 @@ FEATURES = 512
 GATES = 3
 CHUNKS = FEATURES // P
 NODE_TILES = NODES // P
+WARM_UP_MATMULS = 4
 SEPARATE_LOADS = 2
 FIRST_PRODUCT_STEP = 3
 OPERANDS = DIRECTIONS * GATES
@@ -38,6 +39,22 @@ BYTES = (
     + 2 * GATES * FEATURES * FEATURES
     + 4 * DIRECTIONS * NODES * FEATURES
 )
+
+
+def by_pair(bank):
+    return bank[:].rearrange("p t (m e) -> p m t e", e=2)
+
+
+def by_pair_node(bank):
+    return bank[:].rearrange("p t (m e) -> p m e t", e=2)
+
+
+def split_nodes(view):
+    return view.rearrange("p (m e) t -> p m e t", e=2)
+
+
+def pairs_by_node(view):
+    return view.rearrange("p m t e -> p m e t")
 
 
 def by_node(bank):
@@ -62,6 +79,9 @@ def tile_graphconvolution_pb_v_kernel(
         make_identity(nc, identity[:])
         identity_bf16 = once.tile([P, P], BF16, name="identity_bf16")
         make_identity(nc, identity_bf16[:])
+
+        minus_identity = once.tile([P, P], F32, name="minus_identity")
+        nc.scalar.mul(minus_identity[:], identity[:], -1.0)
 
         waiting = []
         x_rows = {}
@@ -151,15 +171,16 @@ def tile_graphconvolution_pb_v_kernel(
             engine.tensor_tensor(out=grad_t[:], in0=rows["grad"][:], in1=rows["t"][:], op=ALU.mult)
             prepared[i]["grad_t"] = grad_t
 
-        def transposed(bank_name, rows):
+        def transposed(bank_name, rows, plain=True):
             bank = psum.tile([P, CHUNKS, P], F32, name=bank_name)
-            nc.tensor.matmul(bank[:, 0, :], lhsT=rows[:, 0:P], rhs=identity[:], start=True, stop=True)
-            for chunk in range(1, CHUNKS):
+            if plain:
+                nc.tensor.matmul(bank[:, 0, :], lhsT=rows[:, 0:P], rhs=identity[:], start=True, stop=True)
+            for chunk in range(1 if plain else 0, CHUNKS):
                 nc.tensor.transpose(bank[:, chunk, :], rows[:, chunk * P : (chunk + 1) * P], identity[:])
             return bank
 
         def fill_c(i, d):
-            banks["c", d] = transposed("a%d" % d, loaded[i]["c"][d][:])
+            banks["c", d] = transposed("a%d" % d, loaded[i]["c"][d][:], plain=(d != 0))
 
         def fill_c_sum(i):
             bank = psum.tile([P, CHUNKS, P], F32, name="a0")
@@ -170,22 +191,31 @@ def tile_graphconvolution_pb_v_kernel(
                         lhsT=loaded[i]["c"][d][:, chunk * P : (chunk + 1) * P],
                         rhs=identity[:],
                         is_transpose=True,
-                        start=(d == 0),
-                        stop=(d == DIRECTIONS - 1),
+                        start=(chunk == 0 and d == 0),
+                        stop=False,
                     )
             banks["c_sum"] = bank
 
+        def take_off_c_sum(pairs):
+            nc.tensor.matmul(
+                banks["c_sum"][:].rearrange("p t (m e) -> p t m e", e=2),
+                lhsT=minus_identity[:],
+                rhs=pairs[:].rearrange("p m t e -> p t m e"),
+                start=False,
+                stop=True,
+            )
+
         def fill_grad_t(i):
-            banks["grad_t"] = transposed("a1", prepared[i]["grad_t"][:])
+            banks["grad_t"] = transposed("a1", prepared[i]["grad_t"][:], plain=False)
 
         def fill_c_squared(i, d):
-            banks["c_squared", d] = transposed("a%d" % d, prepared[i]["c_squared"][d][:])
+            banks["c_squared", d] = transposed("a%d" % d, prepared[i]["c_squared"][d][:], plain=True)
 
         def fill_z(i, d):
-            banks["z", d] = transposed("b%d" % d, loaded[i]["z"][d][:])
+            banks["z", d] = transposed("b%d" % d, loaded[i]["z"][d][:], plain=True)
 
         def fill_r_factor(i, d):
-            banks["r_factor", d] = transposed("b%d" % d, prepared[i]["r_factor"][:, d, :])
+            banks["r_factor", d] = transposed("b%d" % d, prepared[i]["r_factor"][:, d, :], plain=(d == 2))
 
         def turn_h(i):
             bank = psum_pair.tile([P, CHUNKS, P], BF16, name="pair")
@@ -196,8 +226,8 @@ def tile_graphconvolution_pb_v_kernel(
             banks["h"] = bank
 
         def fetch_h(i):
-            h = two.tile([P, P, CHUNKS], BF16, name="h")
-            nc.scalar.copy(out=h[:], in_=by_node(banks["h"]))
+            h = two.tile([P, P // 2, CHUNKS, 2], BF16, name="h")
+            nc.scalar.copy(out=h[:], in_=by_pair(banks["h"]))
             state[i]["h"] = h
 
         w_rows = once.tile([P, GATES, CHUNKS, FEATURES], BF16, name="w_rows")
@@ -277,8 +307,8 @@ def tile_graphconvolution_pb_v_kernel(
                 turn_h(following)
             ec = []
             for d in range(DIRECTIONS):
-                difference = three.tile([P, P, CHUNKS], F32, name="ec")
-                nc.vector.tensor_tensor(out=difference[:], in0=by_node(banks["c", d]), in1=mine["h"][:], op=ALU.subtract)
+                difference = three.tile([P, P // 2, CHUNKS, 2], F32, name="ec")
+                nc.vector.tensor_tensor(out=difference[:], in0=by_pair(banks["c", d]), in1=mine["h"][:], op=ALU.subtract)
                 ec.append(difference)
             fill_c_sum(i)
             if i > 0:
@@ -293,9 +323,10 @@ def tile_graphconvolution_pb_v_kernel(
             for g in REGROUP.get((i, "A"), ()):
                 regroup_weights(g)
             for d in range(DIRECTIONS):
-                zec = six.tile([P, P, CHUNKS], F32, name="zec")
-                nc.vector.tensor_tensor(out=zec[:], in0=by_node(banks["z", d]), in1=ec[d][:], op=ALU.mult)
+                zec = six.tile([P, P // 2, CHUNKS, 2], F32, name="zec")
+                nc.vector.tensor_tensor(out=zec[:], in0=by_pair(banks["z", d]), in1=ec[d][:], op=ALU.mult)
                 mine["zec"].append(zec)
+            take_off_c_sum(mine["zec"][0])
 
             if i == FIRST_PRODUCT_STEP:
                 quantise_weights()
@@ -312,11 +343,10 @@ def tile_graphconvolution_pb_v_kernel(
             if i == 0:
                 prepare_grad_t(0, nc.vector)
                 fill_grad_t(0)
-            zec_sum = two.tile([P, P, CHUNKS], F32, name="zec_sum")
-            nc.vector.tensor_tensor(out=zec_sum[:], in0=mine["zec"][0][:], in1=mine["zec"][1][:], op=ALU.add)
             if i >= 1:
                 quantise(i - 1, 0)
-            nc.vector.tensor_tensor(out=zec_sum[:], in0=zec_sum[:], in1=mine["zec"][2][:], op=ALU.add)
+            zec_sum = two.tile([P, P // 2, CHUNKS, 2], F32, name="zec_sum")
+            nc.vector.tensor_tensor(out=zec_sum[:], in0=mine["zec"][1][:], in1=mine["zec"][2][:], op=ALU.add)
             if i == 0:
                 r_product_by_vector(0, 0)
             if i >= 1:
@@ -326,15 +356,17 @@ def tile_graphconvolution_pb_v_kernel(
             for g in REGROUP.get((i, "B"), ()):
                 regroup_weights(g)
 
-            positive = once.tile([P, P, CHUNKS], F32, name="positive_or_grad_t")
-            nc.vector.tensor_tensor(out=positive[:], in0=by_node(banks["c_sum"]), in1=zec_sum[:], op=ALU.is_gt)
+            positive = once.tile([P, P // 2, CHUNKS, 2], F32, name="positive_or_grad_t")
+            nc.vector.tensor_tensor(out=positive[:], in0=by_pair(banks["c_sum"]), in1=zec_sum[:], op=ALU.is_gt)
             fill_c_squared(i, 0)
             if i == 0:
                 r_product_by_vector(0, 1)
             if i >= 1:
                 quantise(i - 1, 2)
             ds = two.tile([P, P, CHUNKS], F32, name="ds")
-            nc.vector.tensor_tensor(out=ds[:], in0=by_node(banks["grad_t"]), in1=positive[:], op=ALU.mult)
+            nc.vector.tensor_tensor(
+                out=split_nodes(ds[:]), in0=by_pair_node(banks["grad_t"]), in1=pairs_by_node(positive[:]), op=ALU.mult
+            )
             fill_c_squared(i, 1)
             if i == 0:
                 r_product_by_vector(0, 2)
@@ -354,7 +386,12 @@ def tile_graphconvolution_pb_v_kernel(
                 )
                 mine["p"].append(p)
                 fill_r_factor(i, d)
-                nc.gpsimd.tensor_tensor(out=dgi[:, DZ_AT + d], in0=p[:], in1=mine["zec"][d][:], op=ALU.mult)
+                nc.gpsimd.tensor_tensor(
+                    out=split_nodes(dgi[:, DZ_AT + d]),
+                    in0=split_nodes(p[:]),
+                    in1=pairs_by_node(mine["zec"][d][:]),
+                    op=ALU.mult,
+                )
             if not is_last:
                 prepare_products(following, ALL)
 
@@ -399,6 +436,9 @@ def tile_graphconvolution_pb_v_kernel(
 
         ctx.enter_context(tc.manual_schedule())
 
+        warm_up = psum_pair.tile([P, P], F32, name="pair")
+        for turn in range(WARM_UP_MATMULS):
+            nc.tensor.matmul(warm_up[:], lhsT=identity[:], rhs=identity[:], start=True, stop=True)
         load(0)
         turn_h(0)
         fetch_h(0)

from contextlib import ExitStack

import concourse.mybir as mybir
from concourse.masks import make_identity

F32 = mybir.dt.float32
BF16 = mybir.dt.bfloat16
U32 = mybir.dt.uint32
U8 = mybir.dt.uint8
E5M2_X4 = mybir.dt.float8_e5m2_x4
E4M3_X4 = mybir.dt.float8_e4m3fn_x4
ALU = mybir.AluOpType
FUNC = mybir.ActivationFunctionType

P = 128
DIRECTIONS = 3
NODES = 1024
FEATURES = 512
GATES = 3
CHUNKS = FEATURES // P
NODE_TILES = NODES // P
WARM_UP_MATMULS = 4
SEPARATE_LOADS = 2
FIRST_PRODUCT_STEP = 3
OPERANDS = DIRECTIONS * GATES
GATE_AT = (1, 2, 0)
DZ_AT, DC_AT, DR_AT = 0, DIRECTIONS, 2 * DIRECTIONS
QUANTISE_CALLS = ((0, 4), (4, 2), (6, 2), (8, 1))

R_COLS = slice(0, FEATURES)
Z_COLS = slice(FEATURES, 2 * FEATURES)
C_COLS = slice(2 * FEATURES, 3 * FEATURES)

FLOPS = 2 * DIRECTIONS * NODES * GATES * FEATURES * FEATURES
BYTES = (
    4 * DIRECTIONS * NODES * GATES * FEATURES
    + 2 * 4 * NODES * FEATURES
    + 2 * 2 * NODES * FEATURES
    + 2 * GATES * FEATURES * FEATURES
    + 4 * DIRECTIONS * NODES * FEATURES
)


def by_pair(bank):
    return bank[:].rearrange("p t (m e) -> p m t e", e=2)


def by_pair_node(bank):
    return bank[:].rearrange("p t (m e) -> p m e t", e=2)


def split_nodes(view):
    return view.rearrange("p (m e) t -> p m e t", e=2)


def pairs_by_node(view):
    return view.rearrange("p m t e -> p m e t")


def by_node(bank):
    return bank[:].rearrange("p t n -> p n t")


def tile_graphconvolution_pb_v_kernel(
    tc, agg, x, wih, whh, bih, bhh, wh, bh, gates, hn, t, grad_out, out
):
    nc = tc.nc
    ALL = slice(0, DIRECTIONS)
    REGROUP = {(1, "C"): (0,), (2, "A"): (1,), (2, "B"): (2,)}
    with ExitStack() as ctx:
        once = ctx.enter_context(tc.tile_pool(name="once", bufs=1))
        two = ctx.enter_context(tc.tile_pool(name="two", bufs=2))
        three = ctx.enter_context(tc.tile_pool(name="three", bufs=DIRECTIONS))
        six = ctx.enter_context(tc.tile_pool(name="six", bufs=2 * DIRECTIONS))
        psum = ctx.enter_context(tc.psum_pool(name="psum", bufs=1))
        psum_pair = ctx.enter_context(tc.psum_pool(name="psum_pair", bufs=2))

        identity = once.tile([P, P], F32, name="identity")
        make_identity(nc, identity[:])
        identity_bf16 = once.tile([P, P], BF16, name="identity_bf16")
        make_identity(nc, identity_bf16[:])

        minus_identity = once.tile([P, P], F32, name="minus_identity")
        nc.scalar.mul(minus_identity[:], identity[:], -1.0)

        waiting = []
        x_rows = {}
        loaded = {}
        prepared = {}
        banks = {}
        state = {}

        def load(i):
            rows = slice(i * P, (i + 1) * P)
            tiles = {}

            def fetch(pool, name, dtype, source):
                tile = pool.tile([P, FEATURES], dtype, name=name + "_rows")
                nc.sync.dma_start(out=tile[:], in_=source)
                return tile

            def gate(name, cols):
                tile = two.tile([P, DIRECTIONS, FEATURES], F32, name=name + "_rows")
                if i < SEPARATE_LOADS:
                    for d in range(DIRECTIONS):
                        nc.sync.dma_start(out=tile[:, d, :], in_=gates[d, 0, rows, cols])
                else:
                    nc.sync.dma_start(out=tile[:], in_=gates[:, 0, rows, cols].rearrange("d n f -> n d f"))
                return [tile[:, d, :] for d in range(DIRECTIONS)]

            def product_inputs():
                tiles["grad"] = fetch(two, "grad", BF16, grad_out[rows, 0, :])
                tiles["t"] = fetch(two, "t", F32, t[rows, 0, :])

            def load_x(j):
                x_rows[j] = fetch(two, "x", BF16, x[j * P : (j + 1) * P, 0, :])

            if i > 0:
                product_inputs()
            if i not in x_rows:
                load_x(i)
            tiles["x"] = x_rows[i]
            tiles["c"] = gate("c", C_COLS)
            if i == 0:
                load_x(1)
            if i == 0:
                tiles["z"] = gate("z", Z_COLS)
                product_inputs()
            tiles["hn"] = fetch(two, "hn", F32, hn[0, rows, :])
            tiles["r"] = gate("r", R_COLS)
            if i > 0:
                tiles["z"] = gate("z", Z_COLS)
            loaded[i] = tiles
            prepared[i] = {"c_squared": []}
            state[i] = {"zec": [], "p": []}

        def prepare_squares(i):
            rows = loaded[i]
            for d in range(DIRECTIONS):
                c_sq = six.tile([P, FEATURES], F32, name="c_squared")
                nc.scalar.square(c_sq[:], rows["c"][d][:])
                prepared[i]["c_squared"].append(c_sq)
            prepared[i]["r_factor"] = two.tile([P, DIRECTIONS, FEATURES], F32, name="r_factor")

        def some_directions(which):
            return range(which.start, which.stop)

        def square_r(i, d):
            factor = prepared[i]["r_factor"]
            nc.scalar.activation(out=factor[:, d, :], in_=loaded[i]["r"][d][:], func=FUNC.Square, bias=-0.5, scale=1.0)

        def prepare_r_factor(i, which):
            factor = prepared[i]["r_factor"]
            for d in some_directions(which):
                nc.scalar.activation(out=factor[:, d, :], in_=factor[:, d, :], func=FUNC.Copy, scale=-1.0, bias=0.25)

        def prepare_products(i, which):
            factor = prepared[i]["r_factor"][:, which, :]
            hn_for_each = loaded[i]["hn"][:].unsqueeze(1).to_broadcast([P, which.stop - which.start, FEATURES])
            nc.gpsimd.tensor_tensor(out=factor, in0=factor, in1=hn_for_each, op=ALU.mult)

        def r_product_by_vector(i, d):
            factor = prepared[i]["r_factor"][:, d, :]
            nc.vector.scalar_tensor_tensor(
                out=factor, in0=factor, scalar=0.25, in1=loaded[i]["hn"][:], op0=ALU.subtract, op1=ALU.mult
            )

        def prepare_grad_t(i, engine):
            rows = loaded[i]
            grad_t = once.tile([P, FEATURES], F32, name="positive_or_grad_t")
            engine.tensor_tensor(out=grad_t[:], in0=rows["grad"][:], in1=rows["t"][:], op=ALU.mult)
            prepared[i]["grad_t"] = grad_t

        def transposed(bank_name, rows, plain=True):
            bank = psum.tile([P, CHUNKS, P], F32, name=bank_name)
            if plain:
                nc.tensor.matmul(bank[:, 0, :], lhsT=rows[:, 0:P], rhs=identity[:], start=True, stop=True)
            for chunk in range(1 if plain else 0, CHUNKS):
                nc.tensor.transpose(bank[:, chunk, :], rows[:, chunk * P : (chunk + 1) * P], identity[:])
            return bank

        def fill_c(i, d):
            banks["c", d] = transposed("a%d" % d, loaded[i]["c"][d][:], plain=(d != 0))

        def fill_c_sum(i):
            bank = psum.tile([P, CHUNKS, P], F32, name="a0")
            for chunk in range(CHUNKS):
                for d in range(DIRECTIONS):
                    nc.tensor.matmul(
                        bank[:, chunk, :],
                        lhsT=loaded[i]["c"][d][:, chunk * P : (chunk + 1) * P],
                        rhs=identity[:],
                        is_transpose=True,
                        start=(chunk == 0 and d == 0),
                        stop=False,
                    )
            banks["c_sum"] = bank

        def take_off_c_sum(pairs):
            nc.tensor.matmul(
                banks["c_sum"][:].rearrange("p t (m e) -> p t m e", e=2),
                lhsT=minus_identity[:],
                rhs=pairs[:].rearrange("p m t e -> p t m e"),
                start=False,
                stop=True,
            )

        def fill_grad_t(i):
            banks["grad_t"] = transposed("a1", prepared[i]["grad_t"][:], plain=False)

        def fill_c_squared(i, d):
            banks["c_squared", d] = transposed("a%d" % d, prepared[i]["c_squared"][d][:], plain=True)

        def fill_z(i, d):
            banks["z", d] = transposed("b%d" % d, loaded[i]["z"][d][:], plain=True)

        def fill_r_factor(i, d):
            banks["r_factor", d] = transposed("b%d" % d, prepared[i]["r_factor"][:, d, :], plain=(d == 2))

        def turn_h(i):
            bank = psum_pair.tile([P, CHUNKS, P], BF16, name="pair")
            for chunk in range(CHUNKS):
                nc.tensor.transpose(
                    bank[:, chunk, :], loaded[i]["x"][:, chunk * P : (chunk + 1) * P], identity_bf16[:]
                )
            banks["h"] = bank

        def fetch_h(i):
            h = two.tile([P, P // 2, CHUNKS, 2], BF16, name="h")
            nc.scalar.copy(out=h[:], in_=by_pair(banks["h"]))
            state[i]["h"] = h

        w_rows = once.tile([P, GATES, CHUNKS, FEATURES], BF16, name="w_rows")
        w_grouped = once.tile([P, GATES, FEATURES, CHUNKS], BF16, name="w_grouped", align_bytes=64)
        w_codes = once.tile([P, GATES, FEATURES], U32, name="w_codes", align_bytes=64)
        w_scales = once.tile([P, GATES, FEATURES], U8, name="w_scales", align_bytes=64)

        def load_weights():
            nc.sync.dma_start(
                out=w_rows[:], in_=wih.rearrange("(g t p) n -> p g t n", t=CHUNKS, p=P)
            )

        def regroup_weights(g):
            nc.scalar.copy(out=w_grouped[:, g], in_=w_rows[:, g].rearrange("p t n -> p n t"))

        def quantise_weights():
            for g in range(GATES):
                nc.vector.quantize_mx(
                    out=w_codes[:, g, :].bitcast(E4M3_X4),
                    scales=w_scales[:, g, :],
                    in_=w_grouped[:, g].rearrange("p n t -> p (n t)"),
                )

        def quantise(i, call):
            first, count = QUANTISE_CALLS[call]
            if first == 0:
                state[i]["codes"] = three.tile([P, OPERANDS, P], U32, name="codes", align_bytes=64)
                state[i]["scales"] = three.tile([P, OPERANDS, P], U8, name="scales", align_bytes=64)
            some = slice(first, first + count)
            nc.vector.quantize_mx(
                out=state[i]["codes"][:, some, :].rearrange("p u n -> p (u n)").bitcast(E5M2_X4),
                scales=state[i]["scales"][:, some, :].rearrange("p u n -> p (u n)"),
                in_=state[i]["dgi"][:, some].rearrange("p u n t -> p (u n t)"),
            )

        def product_pass(i, d, place, acc):
            g = GATE_AT[place]
            nc.tensor.matmul_mx(
                out=acc[:],
                lhsT=state[i]["codes"][:, DIRECTIONS * place + d, :].bitcast(E5M2_X4),
                lhsT_scale=state[i]["scales"][:, DIRECTIONS * place + d, :],
                rhs=w_codes[:, g, :].bitcast(E4M3_X4),
                rhs_scale=w_scales[:, g, :],
                start=(place == 0),
                stop=(place == GATES - 1),
            )

        def store(i, d, acc, by_vector=False):
            result = six.tile([P, FEATURES], F32, name="result")
            if by_vector:
                nc.vector.tensor_copy(out=result[:], in_=acc[:])
            else:
                nc.scalar.copy(out=result[:], in_=acc[:])
            nc.sync.dma_start(out=out[d, 0, i * P : (i + 1) * P, :], in_=result[:])

        def multiply(i, d):
            acc = psum_pair.tile([P, FEATURES], F32, name="pair")
            for place in range(GATES):
                product_pass(i, d, place, acc)
            store(i, d, acc)

        def quantise_and_multiply(i, call, accs):
            quantise(i, call)
            first, count = QUANTISE_CALLS[call]
            for operand in range(first, first + count):
                place, d = divmod(operand, DIRECTIONS)
                product_pass(i, d, place, accs[d])
                if place == GATES - 1:
                    store(i, d, accs[d], by_vector=(d == DIRECTIONS - 1))

        def gradient(i):
            following = i + 1
            is_last = following == NODE_TILES
            mine = state[i]

            if not is_last:
                turn_h(following)
            ec = []
            for d in range(DIRECTIONS):
                difference = three.tile([P, P // 2, CHUNKS, 2], F32, name="ec")
                nc.vector.tensor_tensor(out=difference[:], in0=by_pair(banks["c", d]), in1=mine["h"][:], op=ALU.subtract)
                ec.append(difference)
            fill_c_sum(i)
            if i > 0:
                fill_grad_t(i)
            fill_c_squared(i, 2)
            if 0 < i < NODE_TILES - 2:
                load(i + 2)
            if not is_last:
                prepare_squares(following)
                fetch_h(following)

            for g in REGROUP.get((i, "A"), ()):
                regroup_weights(g)
            for d in range(DIRECTIONS):
                zec = six.tile([P, P // 2, CHUNKS, 2], F32, name="zec")
                nc.vector.tensor_tensor(out=zec[:], in0=by_pair(banks["z", d]), in1=ec[d][:], op=ALU.mult)
                mine["zec"].append(zec)
            take_off_c_sum(mine["zec"][0])

            if i == FIRST_PRODUCT_STEP:
                quantise_weights()
            if i >= 2:
                waiting.extend((i - 2, d) for d in range(DIRECTIONS))
            turns = min(len(waiting), 4) if i >= FIRST_PRODUCT_STEP else 0
            for turn in range(max(turns, DIRECTIONS)):
                if turn < turns:
                    multiply(*waiting[turn])
                if not is_last and turn < DIRECTIONS:
                    square_r(following, turn)
            waiting[:] = waiting[turns:]

            if i == 0:
                prepare_grad_t(0, nc.vector)
                fill_grad_t(0)
            if i >= 1:
                quantise(i - 1, 0)
            zec_sum = two.tile([P, P // 2, CHUNKS, 2], F32, name="zec_sum")
            nc.vector.tensor_tensor(out=zec_sum[:], in0=mine["zec"][1][:], in1=mine["zec"][2][:], op=ALU.add)
            if i == 0:
                r_product_by_vector(0, 0)
            if i >= 1:
                quantise(i - 1, 1)
            if not is_last:
                prepare_r_factor(following, ALL)
            for g in REGROUP.get((i, "B"), ()):
                regroup_weights(g)

            positive = once.tile([P, P // 2, CHUNKS, 2], F32, name="positive_or_grad_t")
            nc.vector.tensor_tensor(out=positive[:], in0=by_pair(banks["c_sum"]), in1=zec_sum[:], op=ALU.is_gt)
            fill_c_squared(i, 0)
            if i == 0:
                r_product_by_vector(0, 1)
            if i >= 1:
                quantise(i - 1, 2)
            ds = two.tile([P, P, CHUNKS], F32, name="ds")
            nc.vector.tensor_tensor(
                out=split_nodes(ds[:]), in0=by_pair_node(banks["grad_t"]), in1=pairs_by_node(positive[:]), op=ALU.mult
            )
            fill_c_squared(i, 1)
            if i == 0:
                r_product_by_vector(0, 2)
                load(2)
                load_weights()
            if i >= 1:
                quantise(i - 1, 3)
            if not is_last:
                prepare_grad_t(following, nc.gpsimd)

            dgi = two.tile([P, OPERANDS, P, CHUNKS], BF16, name="dgi", align_bytes=64)
            mine["dgi"] = dgi
            for d in range(DIRECTIONS):
                p = three.tile([P, P, CHUNKS], F32, name="p")
                nc.vector.scalar_tensor_tensor(
                    out=p[:], in0=by_node(banks["z", d]), scalar=1.0, in1=ds[:], op0=ALU.subtract, op1=ALU.mult
                )
                mine["p"].append(p)
                fill_r_factor(i, d)
                nc.gpsimd.tensor_tensor(
                    out=split_nodes(dgi[:, DZ_AT + d]),
                    in0=split_nodes(p[:]),
                    in1=pairs_by_node(mine["zec"][d][:]),
                    op=ALU.mult,
                )
            if not is_last:
                prepare_products(following, ALL)

            dc_f32 = []
            for d in range(DIRECTIONS):
                dc_exact = three.tile([P, P, CHUNKS], F32, name="dc_exact")
                nc.vector.scalar_tensor_tensor(
                    out=dc_exact[:],
                    in0=by_node(banks["c_squared", d]),
                    scalar=1.0,
                    in1=mine["p"][d][:],
                    op0=ALU.subtract,
                    op1=ALU.mult,
                )
                dc_f32.append(dc_exact)
                nc.scalar.copy(out=dgi[:, DC_AT + d], in_=dc_exact[:])
                if not is_last:
                    fill_c(following, d)

            for g in REGROUP.get((i, "C"), ()):
                regroup_weights(g)
            if is_last:
                for d in range(DIRECTIONS):
                    multiply(i - 1, d)
                accs = [psum.tile([P, FEATURES], F32, name="a%d" % d) for d in range(DIRECTIONS)]
            for d in range(DIRECTIONS):
                if i == 0:
                    nc.vector.scalar_tensor_tensor(
                        out=dgi[:, DR_AT + d], in0=by_node(banks["r_factor", d]), scalar=-1.0, in1=dc_f32[d][:], op0=ALU.mult, op1=ALU.mult
                    )
                else:
                    nc.vector.tensor_tensor(
                        out=dgi[:, DR_AT + d], in0=by_node(banks["r_factor", d]), in1=dc_f32[d][:], op=ALU.mult
                    )
                if not is_last:
                    fill_z(following, d)
                elif d >= 1:
                    quantise_and_multiply(i, d - 1, accs)
            if is_last:
                quantise_and_multiply(i, 2, accs)
                quantise_and_multiply(i, 3, accs)

        ctx.enter_context(tc.manual_schedule())

        warm_up = psum_pair.tile([P, P], F32, name="pair")
        for turn in range(WARM_UP_MATMULS):
            nc.tensor.matmul(warm_up[:], lhsT=identity[:], rhs=identity[:], start=True, stop=True)
        load(0)
        turn_h(0)
        fetch_h(0)
        for d in range(DIRECTIONS):
            fill_c(0, d)
        for d in range(DIRECTIONS):
            fill_z(0, d)
        prepare_squares(0)
        for d in range(DIRECTIONS):
            square_r(0, d)
        load(1)

        gradient(0)
        for i in range(1, NODE_TILES):
            gradient(i)
